import numpy as np
import ml_dtypes


def mxq(x, axis, fmt="e4m3"):
    dtype, down = {"e4m3": (ml_dtypes.float8_e4m3fn, 7), "e5m2": (ml_dtypes.float8_e5m2, 14)}[fmt]
    v = np.moveaxis(np.asarray(x, np.float32).astype(ml_dtypes.bfloat16).astype(np.float64), axis, -1)
    blocks = v.reshape(v.shape[:-1] + (-1, 32))
    amax = np.abs(blocks).max(-1, keepdims=True)
    byte = np.maximum(np.where(amax > 0, np.frexp(amax)[1] - 1 + 127, 0) - down, 1)
    scale = np.exp2(byte - 127.0)
    codes = (blocks / scale).astype(np.float32).astype(dtype).astype(np.float64)
    return np.moveaxis((codes * scale).reshape(v.shape), -1, axis)


WIDE = False


def mx_kscale(k):
    if not WIDE:
        return np.ones(k)
    levels = np.array([10, -10, 5, -5, 0])
    if k % 512:
        return np.exp2(np.random.permutation(np.resize(levels, k // 32))).repeat(32)
    a = np.empty((k // 512, 16))
    for p in range(k // 512):
        a[p, :8] = np.random.permutation(np.resize(levels, 8))
        for g in range(8):
            far = levels[np.abs(levels - a[p, g]) >= 10]
            a[p, g + 8] = far[np.random.randint(len(far))]
    return np.exp2(a.ravel()).repeat(32)


BF16 = ml_dtypes.bfloat16


def bf(x):
    return np.asarray(x, np.float32).astype(BF16)


def f64(x):
    return np.asarray(x).astype(np.float64)


N, K, F, H, O, Q, GS, SO = 1024, 8, 1024, 512, 256, 1024, 3, 2


def draw0():
    s, t = mx_kscale(F), mx_kscale(H)
    return {"x": bf(np.random.standard_normal((N, F)) * s),
            "contexts": bf(np.random.standard_normal((N, K, F)) * s),
            "attn": bf(np.random.random((N, K))),
            "Wn": bf(np.random.standard_normal((H, F)) * 0.5 / np.sqrt(F) / s * t[:, None]),
            "bn": bf(np.random.standard_normal(H) * 0.1 * t),
            "Wc": bf(np.random.standard_normal((H, F)) * 1.5 / np.sqrt(F) / s * t[:, None]),
            "bc": bf(np.random.standard_normal(H) * 0.1 * t),
            "Wu": bf(np.random.standard_normal((O, H)) * 1.5 / np.sqrt(H) / t),
            "bu": bf(np.random.standard_normal(O) * 0.1)}


def core(x, contexts, attn, Wn, bn, Wc, bc, Wu, bu):
    xt = (mxq(f64(x), 1, "e4m3") @ mxq(f64(Wn).T, 0, "e4m3")) + f64(bn)
    ct = (mxq(f64(contexts).reshape(N * K, F), 1, "e4m3") @ mxq(f64(Wc).T, 0, "e4m3")).reshape(N, K, H) + f64(bc)
    ca = (ct * f64(attn)[..., None]).mean(axis=1)
    return (mxq(xt + ca, 1, "e4m3") @ mxq(f64(Wu).T, 0, "e4m3")) + f64(bu)


def e4m3fn_bytes(y):
    return np.clip(np.asarray(y, np.float64), -448.0, 448.0).astype(np.float32).astype(ml_dtypes.float8_e4m3fn).view(np.uint8)


def e4m3fn_values(b):
    return np.asarray(b, np.uint8).view(ml_dtypes.float8_e4m3fn).astype(np.float64)


def setup_inputs():
    d = draw0()
    x0 = np.asarray(d['contexts']).astype(np.float64)
    s = (np.max(np.abs(x0), axis=(0, 1), keepdims=True) / 448.0).astype(np.float32)
    out = {}
    for k, v in d.items():
        if k == 'contexts':
            out['contexts_bytes'] = e4m3fn_bytes(x0 / s.astype(np.float64))
            out['contexts_scale'] = s
        else:
            out[k] = v
    return out


def reference(x, contexts_bytes, contexts_scale, attn, Wn, bn, Wc, bc, Wu, bu):
    return core(x, e4m3fn_values(contexts_bytes) * contexts_scale.astype(np.float64), attn, Wn, bn, Wc, bc, Wu, bu)

@@ -1,0 +1,369 @@
+from contextlib import ExitStack
+
+import concourse.mybir as mybir
+from concourse.masks import make_identity
+
+N, K, F, H, O = 1024, 8, 1024, 512, 256
+FLOPS = 2 * (N * F * H + N * K * F * H + N * H * O)
+
+F32 = mybir.dt.float32
+BF16 = mybir.dt.bfloat16
+U32 = mybir.dt.uint32
+U8 = mybir.dt.uint8
+FP8 = mybir.dt.float8_e4m3fn
+FP8X4 = mybir.dt.float8_e4m3fn_x4
+MULT = mybir.AluOpType.mult
+ADD = mybir.AluOpType.add
+COPY = mybir.ActivationFunctionType.Copy
+AXIS_X = mybir.AxisListType.X
+
+P = 128
+TILES = N // P
+RUN = 3
+LEAD = 3
+CTX_PER_LOAD = 2
+
+
+def tile_nodeembeddinglayer_pa_t_kernel(
+    tc, x, contexts_bytes, contexts_scale, attn, Wn, bn, Wc, bc, Wu, bu, out
+):
+    nc = tc.nc
+    with ExitStack() as ctx:
+        keep = ctx.enter_context(tc.tile_pool(name="keep", bufs=1))
+        work = ctx.enter_context(tc.tile_pool(name="work", bufs=1))
+        psum = ctx.enter_context(tc.psum_pool(name="psum", bufs=1))
+        ctx.enter_context(tc.manual_schedule())
+
+        ident = keep.tile([P, P], F32, name="ident")
+        make_identity(nc, ident[:])
+
+        x_rows = x.rearrange("(p j) f -> p j f", j=TILES)
+        ctx_rows = contexts_bytes.rearrange("(p j) k f -> p j (k f)", j=TILES)
+        out_rows = out.rearrange("(p j) o -> p j o", j=TILES)
+        wc_rows = Wc.rearrange("(m t) f -> m t f", t=4)
+        wn_rows = Wn.rearrange("(m t) f -> m t f", t=4)
+        raw = {}
+
+        def load_rows(key, src):
+            tile = keep.tile([P, F], BF16, name="raw_%s%d" % key)
+            nc.sync.dma_start(out=tile[:], in_=src)
+            raw[key] = tile
+
+        def load_ctx(j, k0):
+            tile = keep.tile([P, CTX_PER_LOAD * F], U8, name="ctx_bytes_%d_%d" % (j, k0))
+            nc.sync.dma_start(out=tile[:], in_=ctx_rows[:, j, k0 * F : (k0 + CTX_PER_LOAD) * F])
+            for i in range(CTX_PER_LOAD):
+                raw[("ctx", j, k0 + i)] = tile[:, i * F : (i + 1) * F]
+
+        scale_cols = keep.tile([P, 8], F32, name="scale_cols")
+        nc.sync.dma_start(out=scale_cols[:], in_=contexts_scale.rearrange("a b (n m) -> (a b n) m", m=8))
+        for t in range(4):
+            load_rows(("wc", t), wc_rows[:, t, :])
+        load_ctx(0, 0)
+        attn_sb = keep.tile([P, TILES * K], BF16, name="attn_sb")
+        nc.sync.dma_start(out=attn_sb[:], in_=attn.rearrange("(p j) k -> p (j k)", j=TILES))
+        load_ctx(0, 2)
+        for t in range(4):
+            load_rows(("wn", t), wn_rows[:, t, :])
+        bias_rows = keep.tile([P, H], BF16, name="bias_rows")
+        nc.sync.dma_start(out=bias_rows[0:64, :], in_=bc.partition_broadcast(64))
+        nc.sync.dma_start(out=bias_rows[64:128, :], in_=bn.partition_broadcast(64))
+        load_ctx(0, 4)
+        load_ctx(0, 6)
+        load_rows(("x", 0), x_rows[:, 0, :])
+        wu_raw = keep.tile([P, 2, H], BF16, name="wu_raw")
+        nc.sync.dma_start(out=wu_raw[:], in_=Wu.rearrange("(a p) h -> p a h", p=P))
+        bu_rows = keep.tile([P, O], BF16, name="bu_rows")
+        nc.sync.dma_start(out=bu_rows[:], in_=bu.partition_broadcast(P))
+        for j in range(1, TILES):
+            load_rows(("x", j), x_rows[:, j, :])
+            for k0 in range(0, K, CTX_PER_LOAD):
+                load_ctx(j, k0)
+
+        def turn_bank(n):
+            return psum.tile([P, 512], F32, name="turn", tag="turn%d" % (n % RUN))
+
+        def prod_bank(n):
+            return psum.tile([P, 512], F32, name="prod", tag="prod%d" % (n % RUN))
+
+        def sum_bank(j, width):
+            return psum.tile([P, width], F32, name="hsum", tag="hsum%d" % (j % 2))
+
+        spread = keep.tile([P, F], F32, name="spread")
+        spread_view = spread[:].rearrange("p (u q i m) -> p u q i m", u=2, i=2, m=8)
+        scale_banks = []
+        for half in range(2):
+            bank = prod_bank(half)
+            for m in range(4):
+                col = scale_cols[:, 4 * half + m : 4 * half + m + 1].to_broadcast([P, P])
+                nc.tensor.transpose(bank[:, m * P : (m + 1) * P], col, ident[:])
+            scale_banks.append(bank[:].rearrange("p (m q u i) -> p u q i m", m=4, u=2, i=2))
+
+        def permute_wc(t):
+            tile = keep.tile([P, F], BF16, name="wc_perm%d" % t)
+            nc.vector.tensor_copy(
+                out=tile[:].rearrange("p (u q i) -> p u q i", u=2, i=16),
+                in_=raw[("wc", t)][:].rearrange("p (q u i) -> p u q i", u=2, i=16),
+            )
+            return tile
+
+        block_of_row = keep.tile([P, 16], F32, name="block_of_row")
+        nc.vector.tensor_reduce(
+            out=block_of_row[:], in_=ident[:].rearrange("p (b i) -> p b i", i=8), axis=AXIS_X, op=ADD
+        )
+        weights = keep.tile([P, P], F32, name="weights")
+        nc.vector.memset(weights[:, 64:128], 1.0 / 64)
+        upper = keep.tile([P, 1], F32, name="upper")
+        nc.vector.tensor_reduce(out=upper[:], in_=ident[:, 64:128], axis=AXIS_X, op=ADD)
+        wc_perm = [permute_wc(0)]
+        row_mask = keep.tile([P, TILES], F32, name="row_mask")
+        nc.vector.tensor_scalar(
+            out=row_mask[:], in0=block_of_row[:, 0:TILES], scalar1=upper[:], scalar2=None, op0=ADD
+        )
+        nc.scalar.copy(out=spread_view[:, :, :, :, 0:4], in_=scale_banks[0])
+        wc_perm.append(permute_wc(1))
+        nc.vector.tensor_copy(out=spread_view[:, :, :, :, 4:8], in_=scale_banks[1])
+        wc_perm.append(permute_wc(2))
+        wc_perm.append(permute_wc(3))
+        nc.vector.tensor_scalar(
+            out=weights[:, 0:64], in0=attn_sb[:], scalar1=1.0 / K, scalar2=None, op0=MULT
+        )
+
+        units = [("ctx", 0, 0), ("ctx", 0, 1), ("ctx", 0, 2)]
+        units = units + [("wn", 0, 0), ("ctx", 0, 3), ("wn", 0, 1), ("wn", 0, 2), ("ctx", 0, 4), ("wn", 0, 3)]
+        units = units + [("ctx", 0, 5), ("ctx", 0, 6), ("wu", 0, 0), ("ctx", 0, 7), ("x", 0, 0)]
+        for j in range(1, TILES):
+            units = units + [("ctx", j, k) for k in range(4)] + [("x", j, 0)] + [("ctx", j, k) for k in range(4, K)]
+        runs = [list(range(s, min(s + RUN, len(units)))) for s in range(0, len(units), RUN)]
+        ctx_units = [n for n in range(len(units)) if units[n][0] == "ctx"]
+        last_of_tile = {}
+        first_of_tile = {}
+        for n in range(len(units)):
+            if units[n][0] in ("ctx", "x"):
+                last_of_tile[units[n][1]] = n
+                first_of_tile.setdefault(units[n][1], n)
+
+        scaled, banks, grouped, codes, planes, products, weighted = {}, {}, {}, {}, {}, {}, {}
+        w_grouped = {
+            "wc": keep.tile([P, 2, 2 * H], F32, name="wc_grouped", align_bytes=64),
+            "wn": keep.tile([P, 2, 2 * H], F32, name="wn_grouped", align_bytes=64),
+        }
+        w_codes = {
+            "wc": keep.tile([P, 2, H], U32, name="wc_codes", align_bytes=64),
+            "wn": keep.tile([P, 2, H], U32, name="wn_codes", align_bytes=64),
+        }
+        w_planes = {
+            "wc": keep.tile([P, 2, H], U8, name="wc_plane", align_bytes=64),
+            "wn": keep.tile([P, 2, H], U8, name="wn_plane", align_bytes=64),
+        }
+
+        def scale_ctx(n):
+            tile = work.tile([P, F], BF16, name="scaled", bufs=2 * RUN + LEAD + 1)
+            nc.vector.tensor_tensor(
+                out=tile[:].rearrange("p (u q i) -> p u q i", u=2, i=16),
+                in0=raw[units[n]].bitcast(FP8).rearrange("p (q u i) -> p u q i", u=2, i=16),
+                in1=spread[:].rearrange("p (u q i) -> p u q i", u=2, i=16),
+                op=MULT,
+            )
+            scaled[n] = tile
+
+        def turn(n, src, permuted):
+            words = src.bitcast(F32)
+            bank = turn_bank(n)
+            for g in range(2):
+                for u in range(2):
+                    if permuted:
+                        cols = words[:, 256 * u + P * g : 256 * u + P * (g + 1)]
+                    else:
+                        cols = words[:, 256 * g + u : 256 * (g + 1) : 2]
+                    nc.tensor.transpose(bank[:, (2 * g + u) * P : (2 * g + u + 1) * P], cols, ident[:])
+            return bank[:].rearrange("p (g u r) -> p g r u", g=2, u=2)
+
+        def turn_unit(n):
+            kind, j, k = units[n]
+            if kind == "ctx":
+                banks[n] = turn(n, scaled[n][:], True)
+            elif kind == "x":
+                banks[n] = turn(n, raw[("x", j)][:], False)
+            elif kind == "wn":
+                banks[n] = turn(n, raw[("wn", k)][:], False)
+            else:
+                banks[n] = turn(n, wu_raw[:].rearrange("p a h -> p (a h)"), False)
+
+        def group_weight(kind, t, bank):
+            dst = w_grouped[kind][:, :, 2 * P * t : 2 * P * (t + 1)].rearrange("p g (r u) -> p g r u", u=2)
+            nc.scalar.copy(out=dst, in_=bank)
+
+        def group_unit(n):
+            kind, j, k = units[n]
+            if kind == "wn":
+                group_weight("wn", k, banks[n])
+            else:
+                tile = work.tile([P, 512], F32, name="grouped", bufs=2 * RUN, align_bytes=64)
+                nc.scalar.copy(out=tile[:].rearrange("p (g r u) -> p g r u", g=2, u=2), in_=banks[n])
+                grouped[n] = tile
+
+        def quantize_weight(kind):
+            for g in range(2):
+                nc.vector.quantize_mx(
+                    out=w_codes[kind][:, g, :].bitcast(FP8X4),
+                    scales=w_planes[kind][:, g, :],
+                    in_=w_grouped[kind][:, g, :].bitcast(BF16),
+                )
+
+        def quantize_unit(n):
+            kind, j, k = units[n]
+            if kind == "wn":
+                if k == 3:
+                    quantize_weight("wn")
+                return
+            pool, bufs = (keep, 1) if kind == "wu" else (work, 3 * RUN)
+            codes[n] = pool.tile([P, 256], U32, name="codes", bufs=bufs, align_bytes=64)
+            planes[n] = pool.tile([P, 256], U8, name="plane", bufs=bufs, align_bytes=64)
+            nc.vector.quantize_mx(
+                out=codes[n][:].bitcast(FP8X4), scales=planes[n][:], in_=grouped[n][:].bitcast(BF16)
+            )
+
+        def multiply_unit(n):
+            kind = units[n][0]
+            if kind in ("wn", "wu"):
+                return
+            weight = "wc" if kind == "ctx" else "wn"
+            products[n] = prod_bank(n)
+            for g in range(2):
+                nc.tensor.matmul_mx(
+                    out=products[n][:],
+                    lhsT=codes[n][:, g * P : (g + 1) * P].bitcast(FP8X4),
+                    lhsT_scale=planes[n][:, g * P : (g + 1) * P],
+                    rhs=w_codes[weight][:, g, :].bitcast(FP8X4),
+                    rhs_scale=w_planes[weight][:, g, :],
+                    start=(g == 0),
+                    stop=(g == 1),
+                )
+
+        def weigh_unit(n):
+            kind, j, k = units[n]
+            if kind in ("wn", "wu"):
+                return
+            weighted[n] = work.tile([P, H], F32, name="weighted", bufs=3 * RUN)
+            if kind == "x":
+                nc.scalar.copy(out=weighted[n][:], in_=products[n][:])
+            else:
+                nc.scalar.activation(
+                    out=weighted[n][:], in_=products[n][:], func=COPY, scale=weights[:, K * j + k : K * j + k + 1]
+                )
+
+        sums, masked, h_grouped, h_codes, h_planes, results = {}, {}, {}, {}, {}, {}
+
+        def mask_weights(j):
+            masked[j] = keep.tile([P, P], BF16, name="masked%d" % j)
+            nc.scalar.activation(out=masked[j][:], in_=weights_t[:], func=COPY, scale=row_mask[:, j : j + 1])
+
+        def sum_unit(n):
+            kind, j, k = units[n]
+            if kind in ("wn", "wu"):
+                return
+            if n == first_of_tile[j]:
+                sums[j] = sum_bank(j, H)
+                for t in range(4):
+                    nc.tensor.matmul(
+                        sums[j][:, t * P : (t + 1) * P],
+                        lhsT=bias_cols[:, t * P : (t + 1) * P],
+                        rhs=masked[j][:],
+                        start=(t == 0),
+                        stop=False,
+                    )
+            for t in range(4):
+                nc.tensor.matmul(
+                    sums[j][:, t * P : (t + 1) * P],
+                    lhsT=weighted[n][:, t * P : (t + 1) * P],
+                    rhs=ident[:],
+                    is_transpose=True,
+                    start=False,
+                    stop=(n == last_of_tile[j] and t == 3),
+                )
+
+        def group_h(j):
+            h_grouped[j] = work.tile([P, H], BF16, name="h_grouped", bufs=2, align_bytes=64)
+            nc.scalar.copy(
+                out=h_grouped[j][:].rearrange("p (r t) -> p r t", t=4),
+                in_=sums[j][:].rearrange("p (t r) -> p r t", t=4),
+            )
+
+        def quantize_h(j):
+            h_codes[j] = work.tile([P, P], U32, name="h_codes", bufs=2, align_bytes=64)
+            h_planes[j] = work.tile([P, P], U8, name="h_plane", bufs=2, align_bytes=64)
+            nc.vector.quantize_mx(out=h_codes[j][:].bitcast(FP8X4), scales=h_planes[j][:], in_=h_grouped[j][:])
+
+        def multiply_h(j):
+            wu_unit = units.index(("wu", 0, 0))
+            results[j] = sum_bank(j, O)
+            nc.tensor.matmul_mx(
+                out=results[j][:],
+                lhsT=h_codes[j][:].bitcast(FP8X4),
+                lhsT_scale=h_planes[j][:],
+                rhs=codes[wu_unit][:].bitcast(FP8X4),
+                rhs_scale=planes[wu_unit][:],
+                start=True,
+                stop=True,
+            )
+
+        def finish(j):
+            res = work.tile([P, O], F32, name="res", bufs=2)
+            nc.vector.tensor_tensor(out=res[:], in0=results[j][:], in1=bu_rows[:], op=ADD)
+            nc.sync.dma_start(out=out_rows[:, j, :], in_=res[:])
+
+        for t in range(4):
+            group_weight("wc", t, turn(t, wc_perm[t][:], True))
+        weights_bank = sum_bank(1, P)
+        nc.tensor.transpose(weights_bank[:], weights[:], ident[:])
+        scale_ctx(0)
+        quantize_weight("wc")
+        scale_ctx(1)
+        scale_ctx(2)
+        weights_t = keep.tile([P, P], BF16, name="weights_t")
+        bias_cols = keep.tile([P, H], BF16, name="bias_cols")
+
+        def run(r):
+            return runs[r] if 0 <= r < len(runs) else []
+
+        n_scaled = RUN
+        closed = {}
+        for it in range(-1, len(runs) + 4):
+            need = len([n for n in ctx_units if n < RUN * (it + 3)])
+            goal = min(len(ctx_units), max(need, min(n_scaled + RUN, need + LEAD)))
+            to_scale = ctx_units[n_scaled:goal]
+            n_scaled = goal
+            ahead = 1 if it < 0 else 2
+            for n in to_scale[:ahead]:
+                scale_ctx(n)
+            for n in run(it + 1):
+                turn_unit(n)
+                group_unit(n)
+            if it == 0:
+                nc.scalar.copy(out=weights_t[:], in_=weights_bank[:])
+                nc.scalar.copy(
+                    out=bias_cols[:].rearrange("p (t m) -> p t m", t=4),
+                    in_=bias_rows[:].rearrange("p (m t) -> p t m", t=4),
+                )
+            for n in run(it):
+                if first_of_tile.get(units[n][1]) == n:
+                    mask_weights(units[n][1])
+            for n in run(it - 1):
+                sum_unit(n)
+                if last_of_tile.get(units[n][1]) == n:
+                    group_h(units[n][1])
+                    closed[it] = units[n][1]
+            if it - 1 in closed:
+                quantize_h(closed[it - 1])
+            if it - 2 in closed:
+                finish(closed[it - 2])
+            for n in run(it + 1):
+                quantize_unit(n)
+            for n in to_scale[ahead:]:
+                scale_ctx(n)
+            for n in run(it):
+                multiply_unit(n)
+                weigh_unit(n)
+            if it - 1 in closed:
+                multiply_h(closed[it - 1])

@@ -20,7 +20,31 @@ AXIS_X = mybir.AxisListType.X
 P = 128
 TILES = N // P
 RUN = 3
-LEAD = 3
+HEAD1 = 5
+HEAD2 = 3
+TAIL1 = 2
+TAIL2 = 3
+LEAD = 2
+RING = 3
+XPERM = 1
+FOLD = 0
+FOLD_LAST = 0
+AHEAD = 2
+XPOS = 4
+WN_EARLY = 0
+DLAG = 1
+XAHEAD = 0
+FIN = 1
+RAMP = 0
+GOFF = 1
+SLAG = 1
+FT = 10
+CHAINS = 2
+DEEP_FROM = 99
+FPOS = 0
+WCV = 0
+FEVERY = 1
+ORDER = 0
 CTX_PER_LOAD = 2
 
 
@@ -57,20 +81,20 @@ def tile_nodeembeddinglayer_pa_t_kernel(
 
         scale_cols = keep.tile([P, 8], F32, name="scale_cols")
         nc.sync.dma_start(out=scale_cols[:], in_=contexts_scale.rearrange("a b (n m) -> (a b n) m", m=8))
+        load_ctx(0, 0)
         for t in range(4):
             load_rows(("wc", t), wc_rows[:, t, :])
-        load_ctx(0, 0)
+        load_ctx(0, 2)
         attn_sb = keep.tile([P, TILES * K], BF16, name="attn_sb")
         nc.sync.dma_start(out=attn_sb[:], in_=attn.rearrange("(p j) k -> p (j k)", j=TILES))
-        load_ctx(0, 2)
         for t in range(4):
             load_rows(("wn", t), wn_rows[:, t, :])
+        load_ctx(0, 4)
         bias_rows = keep.tile([P, H], BF16, name="bias_rows")
         nc.sync.dma_start(out=bias_rows[0:64, :], in_=bc.partition_broadcast(64))
         nc.sync.dma_start(out=bias_rows[64:128, :], in_=bn.partition_broadcast(64))
-        load_ctx(0, 4)
-        load_ctx(0, 6)
         load_rows(("x", 0), x_rows[:, 0, :])
+        load_ctx(0, 6)
         wu_raw = keep.tile([P, 2, H], BF16, name="wu_raw")
         nc.sync.dma_start(out=wu_raw[:], in_=Wu.rearrange("(a p) h -> p a h", p=P))
         bu_rows = keep.tile([P, O], BF16, name="bu_rows")
@@ -81,31 +105,24 @@ def tile_nodeembeddinglayer_pa_t_kernel(
                 load_ctx(j, k0)
 
         def turn_bank(n):
-            return psum.tile([P, 512], F32, name="turn", tag="turn%d" % (n % RUN))
+            return psum.tile([P, 512], F32, name="turn", tag="turn%d" % (n % RING))
 
         def prod_bank(n):
-            return psum.tile([P, 512], F32, name="prod", tag="prod%d" % (n % RUN))
+            return psum.tile([P, 512], F32, name="prod", tag="prod%d" % (n % RING))
 
         def sum_bank(j, width):
             return psum.tile([P, width], F32, name="hsum", tag="hsum%d" % (j % 2))
 
         spread = keep.tile([P, F], F32, name="spread")
-        spread_view = spread[:].rearrange("p (u q i m) -> p u q i m", u=2, i=2, m=8)
+        spread_view = spread[:].rearrange("p (u n m) -> p u n m", u=2, m=4)
         scale_banks = []
         for half in range(2):
             bank = prod_bank(half)
             for m in range(4):
-                col = scale_cols[:, 4 * half + m : 4 * half + m + 1].to_broadcast([P, P])
+                first = 4 * (m // 2) + 2 * half + m % 2
+                col = scale_cols[:, first : first + 1].to_broadcast([P, P])
                 nc.tensor.transpose(bank[:, m * P : (m + 1) * P], col, ident[:])
-            scale_banks.append(bank[:].rearrange("p (m q u i) -> p u q i m", m=4, u=2, i=2))
-
-        def permute_wc(t):
-            tile = keep.tile([P, F], BF16, name="wc_perm%d" % t)
-            nc.vector.tensor_copy(
-                out=tile[:].rearrange("p (u q i) -> p u q i", u=2, i=16),
-                in_=raw[("wc", t)][:].rearrange("p (q u i) -> p u q i", u=2, i=16),
-            )
-            return tile
+            scale_banks.append(bank[:].rearrange("p (m n) -> p n m", m=4))
 
         block_of_row = keep.tile([P, 16], F32, name="block_of_row")
         nc.vector.tensor_reduce(
@@ -115,34 +132,53 @@ def tile_nodeembeddinglayer_pa_t_kernel(
         nc.vector.memset(weights[:, 64:128], 1.0 / 64)
         upper = keep.tile([P, 1], F32, name="upper")
         nc.vector.tensor_reduce(out=upper[:], in_=ident[:, 64:128], axis=AXIS_X, op=ADD)
-        wc_perm = [permute_wc(0)]
         row_mask = keep.tile([P, TILES], F32, name="row_mask")
         nc.vector.tensor_scalar(
             out=row_mask[:], in0=block_of_row[:, 0:TILES], scalar1=upper[:], scalar2=None, op0=ADD
         )
-        nc.scalar.copy(out=spread_view[:, :, :, :, 0:4], in_=scale_banks[0])
-        wc_perm.append(permute_wc(1))
-        nc.vector.tensor_copy(out=spread_view[:, :, :, :, 4:8], in_=scale_banks[1])
-        wc_perm.append(permute_wc(2))
-        wc_perm.append(permute_wc(3))
-        nc.vector.tensor_scalar(
-            out=weights[:, 0:64], in0=attn_sb[:], scalar1=1.0 / K, scalar2=None, op0=MULT
-        )
+        nc.scalar.copy(out=spread_view[:, 0], in_=scale_banks[0])
+        nc.vector.tensor_copy(out=spread_view[:, 1], in_=scale_banks[1])
 
-        units = [("ctx", 0, 0), ("ctx", 0, 1), ("ctx", 0, 2)]
-        units = units + [("wn", 0, 0), ("ctx", 0, 3), ("wn", 0, 1), ("wn", 0, 2), ("ctx", 0, 4), ("wn", 0, 3)]
-        units = units + [("ctx", 0, 5), ("ctx", 0, 6), ("wu", 0, 0), ("ctx", 0, 7), ("x", 0, 0)]
+        units = [("wc", 0, t) for t in range(4)] + [("ctx", 0, 0), ("ctx", 0, 1)]
+        for k in range(4):
+            units = units + [("ctx", 0, k + 2), ("wn", 0, k)]
+        units = units + [("wu", 0, 0), ("ctx", 0, 6), ("x", 0, 0), ("ctx", 0, 7)]
         for j in range(1, TILES):
-            units = units + [("ctx", j, k) for k in range(4)] + [("x", j, 0)] + [("ctx", j, k) for k in range(4, K)]
-        runs = [list(range(s, min(s + RUN, len(units)))) for s in range(0, len(units), RUN)]
+            for k in range(K):
+                if k == XPOS and j + XAHEAD < TILES:
+                    units.append(("x", j + XAHEAD, 0))
+                if j == 1 and k < XAHEAD:
+                    units.append(("x", k + 1, 0))
+                units.append(("ctx", j, k))
+        middle = len(units) - HEAD1 - HEAD2 - TAIL1 - TAIL2
+        count = (middle + RUN - 1) // RUN
+        sizes = [HEAD1, HEAD2] + [middle // count + (1 if i < middle % count else 0) for i in range(count)] + [TAIL2, TAIL1]
+        runs = []
+        for size in sizes:
+            first = sum(len(r) for r in runs)
+            runs.append(list(range(first, first + size)))
+        folded = {}
+        for j in range(TILES):
+            mine = [n for n in range(len(units)) if units[n][0] in ("ctx", "x") and units[n][1] == j]
+            for i in range(CHAINS, len(mine)):
+                if mine[i] >= len(units) - FT and units[mine[i]][0] == "ctx":
+                    folded[mine[i]] = mine[i - CHAINS]
         ctx_units = [n for n in range(len(units)) if units[n][0] == "ctx"]
         last_of_tile = {}
         first_of_tile = {}
         for n in range(len(units)):
-            if units[n][0] in ("ctx", "x"):
+            if units[n][0] == "ctx":
                 last_of_tile[units[n][1]] = n
                 first_of_tile.setdefault(units[n][1], n)
 
+        terms = {j: [n for n in range(len(units)) if units[n][0] in ("ctx", "x") and units[n][1] == j and n not in folded.values()] for j in range(TILES)}
+        summed_at = {}
+        for r in range(len(runs)):
+            for n in runs[r]:
+                kind, j, k = units[n]
+                if n in terms[j]:
+                    opens = [q for q in range(len(runs)) if first_of_tile[j] in runs[q]][0]
+                    summed_at.setdefault(max(r, opens) + (2 if n in folded else SLAG), []).append(n)
         scaled, banks, grouped, codes, planes, products, weighted = {}, {}, {}, {}, {}, {}, {}
         w_grouped = {
             "wc": keep.tile([P, 2, 2 * H], F32, name="wc_grouped", align_bytes=64),
@@ -158,14 +194,24 @@ def tile_nodeembeddinglayer_pa_t_kernel(
         }
 
         def scale_ctx(n):
-            tile = work.tile([P, F], BF16, name="scaled", bufs=2 * RUN + LEAD + 1)
+            tile = work.tile([P, F], BF16, name="scaled", bufs=2 * RUN + LEAD + 2)
             nc.vector.tensor_tensor(
-                out=tile[:].rearrange("p (u q i) -> p u q i", u=2, i=16),
-                in0=raw[units[n]].bitcast(FP8).rearrange("p (q u i) -> p u q i", u=2, i=16),
-                in1=spread[:].rearrange("p (u q i) -> p u q i", u=2, i=16),
+                out=tile[:].rearrange("p (u w e) -> p u w e", u=2, e=2),
+                in0=raw[units[n]].bitcast(FP8).rearrange("p (w u e) -> p u w e", u=2, e=2),
+                in1=spread[:].rearrange("p (u w e) -> p u w e", u=2, e=2),
                 op=MULT,
             )
             scaled[n] = tile
+
+        def permute_unit(n):
+            kind, j, k = units[n]
+            if XPERM and kind == "x":
+                src = raw[("x", j)]
+                scaled[n] = work.tile([P, F], BF16, name="permuted", bufs=4)
+                nc.scalar.copy(
+                    out=scaled[n][:].bitcast(F32).rearrange("p (u q i) -> p u q i", u=2, i=1),
+                    in_=src[:].bitcast(F32).rearrange("p (q u i) -> p u q i", u=2, i=1),
+                )
 
         def turn(n, src, permuted):
             words = src.bitcast(F32)
@@ -184,9 +230,9 @@ def tile_nodeembeddinglayer_pa_t_kernel(
             if kind == "ctx":
                 banks[n] = turn(n, scaled[n][:], True)
             elif kind == "x":
-                banks[n] = turn(n, raw[("x", j)][:], False)
-            elif kind == "wn":
-                banks[n] = turn(n, raw[("wn", k)][:], False)
+                banks[n] = turn(n, scaled[n][:] if XPERM else raw[("x", j)][:], XPERM)
+            elif kind in ("wn", "wc"):
+                banks[n] = turn(n, scaled[n][:], True) if n in scaled else turn(n, raw[(kind, k)][:], False)
             else:
                 banks[n] = turn(n, wu_raw[:].rearrange("p a h -> p (a h)"), False)
 
@@ -196,10 +242,10 @@ def tile_nodeembeddinglayer_pa_t_kernel(
 
         def group_unit(n):
             kind, j, k = units[n]
-            if kind == "wn":
-                group_weight("wn", k, banks[n])
+            if kind in ("wn", "wc"):
+                group_weight(kind, k, banks[n])
             else:
-                tile = work.tile([P, 512], F32, name="grouped", bufs=2 * RUN, align_bytes=64)
+                tile = work.tile([P, 512], F32, name="grouped", bufs=RUN + DLAG + 3, align_bytes=64)
                 nc.scalar.copy(out=tile[:].rearrange("p (g r u) -> p g r u", g=2, u=2), in_=banks[n])
                 grouped[n] = tile
 
@@ -213,11 +259,11 @@ def tile_nodeembeddinglayer_pa_t_kernel(
 
         def quantize_unit(n):
             kind, j, k = units[n]
-            if kind == "wn":
+            if kind in ("wn", "wc"):
                 if k == 3:
-                    quantize_weight("wn")
+                    quantize_weight(kind)
                 return
-            pool, bufs = (keep, 1) if kind == "wu" else (work, 3 * RUN)
+            pool, bufs = (keep, 1) if kind == "wu" else (work, 2 * RUN + 1)
             codes[n] = pool.tile([P, 256], U32, name="codes", bufs=bufs, align_bytes=64)
             planes[n] = pool.tile([P, 256], U8, name="plane", bufs=bufs, align_bytes=64)
             nc.vector.quantize_mx(
@@ -226,10 +272,10 @@ def tile_nodeembeddinglayer_pa_t_kernel(
 
         def multiply_unit(n):
             kind = units[n][0]
-            if kind in ("wn", "wu"):
+            if kind in ("wn", "wc", "wu"):
                 return
             weight = "wc" if kind == "ctx" else "wn"
-            products[n] = prod_bank(n)
+            products[n] = prod_bank(len(products))
             for g in range(2):
                 nc.tensor.matmul_mx(
                     out=products[n][:],
@@ -243,10 +289,18 @@ def tile_nodeembeddinglayer_pa_t_kernel(
 
         def weigh_unit(n):
             kind, j, k = units[n]
-            if kind in ("wn", "wu"):
+            if kind in ("wn", "wc", "wu"):
                 return
-            weighted[n] = work.tile([P, H], F32, name="weighted", bufs=3 * RUN)
             if kind == "x":
+                weighted[n] = work.tile([P, H], F32, name="x_product", bufs=XAHEAD + 3)
+            else:
+                weighted[n] = work.tile([P, H], F32, name="weighted", bufs=(SLAG + 1) * RUN + 2)
+            if n in folded:
+                nc.vector.scalar_tensor_tensor(
+                    out=weighted[n][:], in0=products[n][:], scalar=weights[:, K * j + k : K * j + k + 1],
+                    in1=weighted[folded[n]][:], op0=MULT, op1=ADD,
+                )
+            elif kind == "x":
                 nc.scalar.copy(out=weighted[n][:], in_=products[n][:])
             else:
                 nc.scalar.activation(
@@ -260,10 +314,8 @@ def tile_nodeembeddinglayer_pa_t_kernel(
             nc.scalar.activation(out=masked[j][:], in_=weights_t[:], func=COPY, scale=row_mask[:, j : j + 1])
 
         def sum_unit(n):
-            kind, j, k = units[n]
-            if kind in ("wn", "wu"):
-                return
-            if n == first_of_tile[j]:
+            j = units[n][1]
+            if j not in sums:
                 sums[j] = sum_bank(j, H)
                 for t in range(4):
                     nc.tensor.matmul(
@@ -273,6 +325,7 @@ def tile_nodeembeddinglayer_pa_t_kernel(
                         start=(t == 0),
                         stop=False,
                     )
+            terms[j].remove(n)
             for t in range(4):
                 nc.tensor.matmul(
                     sums[j][:, t * P : (t + 1) * P],
@@ -280,7 +333,7 @@ def tile_nodeembeddinglayer_pa_t_kernel(
                     rhs=ident[:],
                     is_transpose=True,
                     start=False,
-                    stop=(n == last_of_tile[j] and t == 3),
+                    stop=(not terms[j] and t == 3),
                 )
 
         def group_h(j):
@@ -297,9 +350,9 @@ def tile_nodeembeddinglayer_pa_t_kernel(
 
         def multiply_h(j):
             wu_unit = units.index(("wu", 0, 0))
-            results[j] = sum_bank(j, O)
+            results[j] = sum_bank(j, H)
             nc.tensor.matmul_mx(
-                out=results[j][:],
+                out=results[j][:, 0:O],
                 lhsT=h_codes[j][:].bitcast(FP8X4),
                 lhsT_scale=h_planes[j][:],
                 rhs=codes[wu_unit][:].bitcast(FP8X4),
@@ -310,36 +363,48 @@ def tile_nodeembeddinglayer_pa_t_kernel(
 
         def finish(j):
             res = work.tile([P, O], F32, name="res", bufs=2)
-            nc.vector.tensor_tensor(out=res[:], in0=results[j][:], in1=bu_rows[:], op=ADD)
+            nc.vector.tensor_tensor(out=res[:], in0=results[j][:, 0:O], in1=bu_rows[:], op=ADD)
             nc.sync.dma_start(out=out_rows[:, j, :], in_=res[:])
 
-        for t in range(4):
-            group_weight("wc", t, turn(t, wc_perm[t][:], True))
-        weights_bank = sum_bank(1, P)
-        nc.tensor.transpose(weights_bank[:], weights[:], ident[:])
-        scale_ctx(0)
-        quantize_weight("wc")
-        scale_ctx(1)
-        scale_ctx(2)
         weights_t = keep.tile([P, P], BF16, name="weights_t")
         bias_cols = keep.tile([P, H], BF16, name="bias_cols")
 
         def run(r):
             return runs[r] if 0 <= r < len(runs) else []
 
-        n_scaled = RUN
+        n_scaled = len([n for n in ctx_units if n in runs[0]])
+        def permute_wc(n):
+            scaled[n] = work.tile([P, F], BF16, name="permuted", bufs=4)
+            nc.vector.tensor_copy(
+                out=scaled[n][:].bitcast(F32).rearrange("p (u w) -> p u w", u=2),
+                in_=raw[("wc", n)][:].bitcast(F32).rearrange("p (w u) -> p u w", u=2),
+            )
+
+        for n in range(4 - WCV, 4):
+            if WCV > 2 and n == 2:
+                scale_ctx(ctx_units[0])
+            permute_wc(n)
+        for n in ctx_units[(1 if WCV > 2 else 0):n_scaled]:
+            scale_ctx(n)
+        for n in run(0):
+            permute_unit(n)
         closed = {}
-        for it in range(-1, len(runs) + 4):
-            need = len([n for n in ctx_units if n < RUN * (it + 3)])
-            goal = min(len(ctx_units), max(need, min(n_scaled + RUN, need + LEAD)))
-            to_scale = ctx_units[n_scaled:goal]
-            n_scaled = goal
-            ahead = 1 if it < 0 else 2
-            for n in to_scale[:ahead]:
-                scale_ctx(n)
-            for n in run(it + 1):
-                turn_unit(n)
-                group_unit(n)
+        n_quantized = 0
+        for it in range(-1, len(runs) + 5):
+            to_turn, to_sum = (run(it + 1) if it < DEEP_FROM else run(it + 1) + run(it + 2) if it == DEEP_FROM else run(it + 2)), summed_at.get(it, [])
+            if it == 0:
+                weights_bank = sum_bank(1, P)
+                nc.tensor.transpose(weights_bank[:], weights[:], ident[:])
+            for i in range(max(len(to_turn), len(to_sum) + GOFF)):
+                if i < len(to_turn):
+                    turn_unit(to_turn[i])
+                    group_unit(to_turn[i])
+                if 0 <= i - GOFF < len(to_sum):
+                    n = to_sum[i - GOFF]
+                    sum_unit(n)
+                    if not terms[units[n][1]]:
+                        group_h(units[n][1])
+                        closed[it] = units[n][1]
             if it == 0:
                 nc.scalar.copy(out=weights_t[:], in_=weights_bank[:])
                 nc.scalar.copy(
@@ -347,23 +412,42 @@ def tile_nodeembeddinglayer_pa_t_kernel(
                     in_=bias_rows[:].rearrange("p (m t) -> p t m", t=4),
                 )
             for n in run(it):
-                if first_of_tile.get(units[n][1]) == n:
+                if n in first_of_tile.values():
                     mask_weights(units[n][1])
-            for n in run(it - 1):
-                sum_unit(n)
-                if last_of_tile.get(units[n][1]) == n:
-                    group_h(units[n][1])
-                    closed[it] = units[n][1]
+            for n in (run(it + 2) if it + 1 < DEEP_FROM else run(it + 2) + run(it + 3) if it + 1 == DEEP_FROM else run(it + 3)):
+                permute_unit(n)
+
+            size = max(len(run(it + 1)), len(run(it + 2)))
+            need = len([n for n in ctx_units if n <= max((run(it + 3) if it + 1 >= DEEP_FROM else []) + run(it + 2) + run(it + 1) + [-1])])
+            goal = min(len(ctx_units), max(need, min(n_scaled + size, need + min(LEAD, max(0, it + RAMP)))))
+            to_scale = ctx_units[n_scaled:goal]
+            n_scaled = max(n_scaled, goal)
+            lag = DLAG if it >= 0 else 0
+            goal = max(max(to_turn + [-1]) + 1 - lag, max(run(it) + [-1]) + 1, n_quantized)
+            to_quantize = list(range(n_quantized, goal))
+            n_quantized = goal
             if it - 1 in closed:
                 quantize_h(closed[it - 1])
-            if it - 2 in closed:
-                finish(closed[it - 2])
-            for n in run(it + 1):
-                quantize_unit(n)
-            for n in to_scale[ahead:]:
-                scale_ctx(n)
-            for n in run(it):
-                multiply_unit(n)
-                weigh_unit(n)
+            slots = max(len(to_scale), len(to_quantize), 1)
+            for i in range(slots):
+                if i < len(to_scale):
+                    scale_ctx(to_scale[i])
+                if it == -1 and i == 0:
+                    nc.vector.tensor_scalar(
+                        out=weights[:, 0:64], in0=attn_sb[:], scalar1=1.0 / K, scalar2=None, op0=MULT
+                    )
+                if i == min(FPOS, slots - 1):
+                    for n in run(it - 1):
+                        if n in folded:
+                            weigh_unit(n)
+                if i == min(FIN, slots - 1) and it - 2 in closed:
+                    finish(closed[it - 2])
+                if i < len(to_quantize):
+                    quantize_unit(to_quantize[i])
+
             if it - 1 in closed:
                 multiply_h(closed[it - 1])
+            for n in run(it):
+                multiply_unit(n)
+                if n not in folded:
+                    weigh_unit(n)

@@ -19,44 +19,37 @@ AXIS_X = mybir.AxisListType.X
 
 P = 128
 TILES = N // P
-RUN = 3
-HEAD1 = 5
-HEAD2 = 3
-TAIL1 = 2
-TAIL2 = 3
-LEAD = 2
-RING = 3
-XPERM = 1
-FOLD = 0
-FOLD_LAST = 0
-AHEAD = 2
-XPOS = 4
-WN_EARLY = 0
-DLAG = 1
-XAHEAD = 0
-FIN = 1
-RAMP = 0
-GOFF = 1
-SLAG = 1
-FT = 10
-CHAINS = 2
-DEEP_FROM = 99
-FPOS = 0
-WCV = 0
-FEVERY = 1
-ORDER = 0
+PACK = 4
+PASSES = F // (P * PACK)
+WORDS = F // 2
+HALF = P // 2
 CTX_PER_LOAD = 2
+
+RUN = 3
+FIRST_RUNS = [5, 2]
+X_PLACE = 4
+LEAD = 1
+CHAINS = 2
 
 
 def tile_nodeembeddinglayer_pa_t_kernel(
     tc, x, contexts_bytes, contexts_scale, attn, Wn, bn, Wc, bc, Wu, bu, out
 ):
     nc = tc.nc
-    with ExitStack() as ctx:
-        keep = ctx.enter_context(tc.tile_pool(name="keep", bufs=1))
-        work = ctx.enter_context(tc.tile_pool(name="work", bufs=1))
-        psum = ctx.enter_context(tc.psum_pool(name="psum", bufs=1))
-        ctx.enter_context(tc.manual_schedule())
+    with ExitStack() as stack:
+        keep = stack.enter_context(tc.tile_pool(name="keep", bufs=1))
+        work = stack.enter_context(tc.tile_pool(name="work", bufs=1))
+        psum = stack.enter_context(tc.psum_pool(name="psum", bufs=1))
+        stack.enter_context(tc.manual_schedule())
+
+        def turn_bank(i):
+            return psum.tile([P, WORDS], F32, name="turn", tag="turn%d" % (i % RUN))
+
+        def product_bank(i):
+            return psum.tile([P, H], F32, name="product", tag="product%d" % (i % RUN))
+
+        def h_bank(j, width):
+            return psum.tile([P, width], F32, name="hsum", tag="hsum%d" % (j % 2))
 
         ident = keep.tile([P, P], F32, name="ident")
         make_identity(nc, ident[:])
@@ -64,16 +57,19 @@ def tile_nodeembeddinglayer_pa_t_kernel(
         x_rows = x.rearrange("(p j) f -> p j f", j=TILES)
         ctx_rows = contexts_bytes.rearrange("(p j) k f -> p j (k f)", j=TILES)
         out_rows = out.rearrange("(p j) o -> p j o", j=TILES)
-        wc_rows = Wc.rearrange("(m t) f -> m t f", t=4)
-        wn_rows = Wn.rearrange("(m t) f -> m t f", t=4)
+        weight_rows = {"wc": Wc.rearrange("(m t) f -> m t f", t=PACK), "wn": Wn.rearrange("(m t) f -> m t f", t=PACK)}
         raw = {}
 
-        def load_rows(key, src):
-            tile = keep.tile([P, F], BF16, name="raw_%s%d" % key)
+        def load_rows(unit, src):
+            tile = keep.tile([P, F], BF16, name="raw_%s_%d_%d" % unit)
             nc.sync.dma_start(out=tile[:], in_=src)
-            raw[key] = tile
+            raw[unit] = tile[:]
 
-        def load_ctx(j, k0):
+        def load_weight(kind):
+            for t in range(PACK):
+                load_rows((kind, 0, t), weight_rows[kind][:, t, :])
+
+        def load_contexts(j, k0):
             tile = keep.tile([P, CTX_PER_LOAD * F], U8, name="ctx_bytes_%d_%d" % (j, k0))
             nc.sync.dma_start(out=tile[:], in_=ctx_rows[:, j, k0 * F : (k0 + CTX_PER_LOAD) * F])
             for i in range(CTX_PER_LOAD):
@@ -81,373 +77,314 @@ def tile_nodeembeddinglayer_pa_t_kernel(
 
         scale_cols = keep.tile([P, 8], F32, name="scale_cols")
         nc.sync.dma_start(out=scale_cols[:], in_=contexts_scale.rearrange("a b (n m) -> (a b n) m", m=8))
-        load_ctx(0, 0)
-        for t in range(4):
-            load_rows(("wc", t), wc_rows[:, t, :])
-        load_ctx(0, 2)
-        attn_sb = keep.tile([P, TILES * K], BF16, name="attn_sb")
-        nc.sync.dma_start(out=attn_sb[:], in_=attn.rearrange("(p j) k -> p (j k)", j=TILES))
-        for t in range(4):
-            load_rows(("wn", t), wn_rows[:, t, :])
-        load_ctx(0, 4)
+        load_contexts(0, 0)
+        load_weight("wc")
+        load_contexts(0, 2)
+        attn_rows = keep.tile([P, TILES * K], BF16, name="attn_rows")
+        nc.sync.dma_start(out=attn_rows[:], in_=attn.rearrange("(p j) k -> p (j k)", j=TILES))
+        load_weight("wn")
+        load_contexts(0, 4)
         bias_rows = keep.tile([P, H], BF16, name="bias_rows")
-        nc.sync.dma_start(out=bias_rows[0:64, :], in_=bc.partition_broadcast(64))
-        nc.sync.dma_start(out=bias_rows[64:128, :], in_=bn.partition_broadcast(64))
-        load_rows(("x", 0), x_rows[:, 0, :])
-        load_ctx(0, 6)
-        wu_raw = keep.tile([P, 2, H], BF16, name="wu_raw")
-        nc.sync.dma_start(out=wu_raw[:], in_=Wu.rearrange("(a p) h -> p a h", p=P))
+        nc.sync.dma_start(out=bias_rows[0:HALF, :], in_=bc.partition_broadcast(HALF))
+        nc.sync.dma_start(out=bias_rows[HALF:P, :], in_=bn.partition_broadcast(HALF))
+        load_rows(("x", 0, 0), x_rows[:, 0, :])
+        load_contexts(0, 6)
+        wu_rows = keep.tile([P, O // P, H], BF16, name="wu_rows")
+        nc.sync.dma_start(out=wu_rows[:], in_=Wu.rearrange("(a p) c -> p a c", p=P))
+        raw[("wu", 0, 0)] = wu_rows[:].rearrange("p a c -> p (a c)")
         bu_rows = keep.tile([P, O], BF16, name="bu_rows")
         nc.sync.dma_start(out=bu_rows[:], in_=bu.partition_broadcast(P))
         for j in range(1, TILES):
-            load_rows(("x", j), x_rows[:, j, :])
+            load_rows(("x", j, 0), x_rows[:, j, :])
             for k0 in range(0, K, CTX_PER_LOAD):
-                load_ctx(j, k0)
-
-        def turn_bank(n):
-            return psum.tile([P, 512], F32, name="turn", tag="turn%d" % (n % RING))
-
-        def prod_bank(n):
-            return psum.tile([P, 512], F32, name="prod", tag="prod%d" % (n % RING))
-
-        def sum_bank(j, width):
-            return psum.tile([P, width], F32, name="hsum", tag="hsum%d" % (j % 2))
+                load_contexts(j, k0)
 
         spread = keep.tile([P, F], F32, name="spread")
-        spread_view = spread[:].rearrange("p (u n m) -> p u n m", u=2, m=4)
+        spread_halves = spread[:].rearrange("p (u n s) -> p u n s", u=2, s=4)
         scale_banks = []
-        for half in range(2):
-            bank = prod_bank(half)
-            for m in range(4):
-                first = 4 * (m // 2) + 2 * half + m % 2
-                col = scale_cols[:, first : first + 1].to_broadcast([P, P])
-                nc.tensor.transpose(bank[:, m * P : (m + 1) * P], col, ident[:])
-            scale_banks.append(bank[:].rearrange("p (m n) -> p n m", m=4))
+        for u in range(2):
+            bank = product_bank(u)
+            for s in range(4):
+                m = 4 * (s // 2) + 2 * u + s % 2
+                column = scale_cols[:, m : m + 1].to_broadcast([P, P])
+                nc.tensor.transpose(bank[:, s * P : (s + 1) * P], column, ident[:])
+            scale_banks.append(bank[:].rearrange("p (s n) -> p n s", s=4))
 
-        block_of_row = keep.tile([P, 16], F32, name="block_of_row")
+        block_of_row = keep.tile([P, P // K], F32, name="block_of_row")
         nc.vector.tensor_reduce(
-            out=block_of_row[:], in_=ident[:].rearrange("p (b i) -> p b i", i=8), axis=AXIS_X, op=ADD
+            out=block_of_row[:], in_=ident[:].rearrange("p (b i) -> p b i", i=K), axis=AXIS_X, op=ADD
         )
-        weights = keep.tile([P, P], F32, name="weights")
-        nc.vector.memset(weights[:, 64:128], 1.0 / 64)
-        upper = keep.tile([P, 1], F32, name="upper")
-        nc.vector.tensor_reduce(out=upper[:], in_=ident[:, 64:128], axis=AXIS_X, op=ADD)
+        gains = keep.tile([P, P], F32, name="gains")
+        nc.vector.memset(gains[:, HALF:P], 1.0 / HALF)
+        is_bn_row = keep.tile([P, 1], F32, name="is_bn_row")
+        nc.vector.tensor_reduce(out=is_bn_row[:], in_=ident[:, HALF:P], axis=AXIS_X, op=ADD)
         row_mask = keep.tile([P, TILES], F32, name="row_mask")
         nc.vector.tensor_scalar(
-            out=row_mask[:], in0=block_of_row[:, 0:TILES], scalar1=upper[:], scalar2=None, op0=ADD
+            out=row_mask[:], in0=block_of_row[:, 0:TILES], scalar1=is_bn_row[:], scalar2=None, op0=ADD
         )
-        nc.scalar.copy(out=spread_view[:, 0], in_=scale_banks[0])
-        nc.vector.tensor_copy(out=spread_view[:, 1], in_=scale_banks[1])
+        nc.scalar.copy(out=spread_halves[:, 0], in_=scale_banks[0])
+        nc.vector.tensor_copy(out=spread_halves[:, 1], in_=scale_banks[1])
+        gains_turned = keep.tile([P, P], BF16, name="gains_turned")
+        bias_cols = keep.tile([P, H], BF16, name="bias_cols")
 
-        units = [("wc", 0, t) for t in range(4)] + [("ctx", 0, 0), ("ctx", 0, 1)]
-        for k in range(4):
-            units = units + [("ctx", 0, k + 2), ("wn", 0, k)]
+        units = [("wc", 0, t) for t in range(PACK)] + [("ctx", 0, 0), ("ctx", 0, 1)]
+        for t in range(PACK):
+            units = units + [("ctx", 0, t + 2), ("wn", 0, t)]
         units = units + [("wu", 0, 0), ("ctx", 0, 6), ("x", 0, 0), ("ctx", 0, 7)]
         for j in range(1, TILES):
-            for k in range(K):
-                if k == XPOS and j + XAHEAD < TILES:
-                    units.append(("x", j + XAHEAD, 0))
-                if j == 1 and k < XAHEAD:
-                    units.append(("x", k + 1, 0))
-                units.append(("ctx", j, k))
-        middle = len(units) - HEAD1 - HEAD2 - TAIL1 - TAIL2
-        count = (middle + RUN - 1) // RUN
-        sizes = [HEAD1, HEAD2] + [middle // count + (1 if i < middle % count else 0) for i in range(count)] + [TAIL2, TAIL1]
-        runs = []
-        for size in sizes:
-            first = sum(len(r) for r in runs)
-            runs.append(list(range(first, first + size)))
-        folded = {}
-        for j in range(TILES):
-            mine = [n for n in range(len(units)) if units[n][0] in ("ctx", "x") and units[n][1] == j]
-            for i in range(CHAINS, len(mine)):
-                if mine[i] >= len(units) - FT and units[mine[i]][0] == "ctx":
-                    folded[mine[i]] = mine[i - CHAINS]
+            contexts = [("ctx", j, k) for k in range(K)]
+            units = units + contexts[:X_PLACE] + [("x", j, 0)] + contexts[X_PLACE:]
+        starts = [0, FIRST_RUNS[0]] + list(range(sum(FIRST_RUNS), len(units), RUN)) + [len(units)]
+        runs = [list(range(starts[r], starts[r + 1])) for r in range(len(starts) - 1)]
         ctx_units = [n for n in range(len(units)) if units[n][0] == "ctx"]
-        last_of_tile = {}
-        first_of_tile = {}
-        for n in range(len(units)):
-            if units[n][0] == "ctx":
-                last_of_tile[units[n][1]] = n
-                first_of_tile.setdefault(units[n][1], n)
+        wu_unit = units.index(("wu", 0, 0))
 
-        terms = {j: [n for n in range(len(units)) if units[n][0] in ("ctx", "x") and units[n][1] == j and n not in folded.values()] for j in range(TILES)}
+        def run(r):
+            return runs[r] if 0 <= r < len(runs) else []
+
+        def has_product(n):
+            return units[n][0] in ("ctx", "x")
+
+        last_terms = [n for n in range(len(units)) if has_product(n) and units[n][1] == TILES - 1]
+        added_to = {
+            last_terms[i]: last_terms[i - CHAINS]
+            for i in range(CHAINS, len(last_terms))
+            if units[last_terms[i]][0] == "ctx"
+        }
+        open_terms = {j: [] for j in range(TILES)}
         summed_at = {}
         for r in range(len(runs)):
             for n in runs[r]:
-                kind, j, k = units[n]
-                if n in terms[j]:
-                    opens = [q for q in range(len(runs)) if first_of_tile[j] in runs[q]][0]
-                    summed_at.setdefault(max(r, opens) + (2 if n in folded else SLAG), []).append(n)
-        scaled, banks, grouped, codes, planes, products, weighted = {}, {}, {}, {}, {}, {}, {}
-        w_grouped = {
-            "wc": keep.tile([P, 2, 2 * H], F32, name="wc_grouped", align_bytes=64),
-            "wn": keep.tile([P, 2, 2 * H], F32, name="wn_grouped", align_bytes=64),
-        }
-        w_codes = {
-            "wc": keep.tile([P, 2, H], U32, name="wc_codes", align_bytes=64),
-            "wn": keep.tile([P, 2, H], U32, name="wn_codes", align_bytes=64),
-        }
-        w_planes = {
-            "wc": keep.tile([P, 2, H], U8, name="wc_plane", align_bytes=64),
-            "wn": keep.tile([P, 2, H], U8, name="wn_plane", align_bytes=64),
-        }
+                if has_product(n) and n not in added_to.values():
+                    open_terms[units[n][1]].append(n)
+                    summed_at.setdefault(r + (2 if n in added_to else 1), []).append(n)
+        pieces = [(t, first, HALF) for t in range(2) for first in (0, HALF)] + [(t, 0, P) for t in range(2, PACK)]
+        bias_pieces = {j: list(pieces) for j in range(TILES)}
 
-        def scale_ctx(n):
-            tile = work.tile([P, F], BF16, name="scaled", bufs=2 * RUN + LEAD + 2)
+        prepared, turned, grouped, codes, scales, products, weighed = {}, {}, {}, {}, {}, {}, {}
+        w_grouped, w_codes, w_scales = {}, {}, {}
+        for kind in ("wc", "wn"):
+            w_grouped[kind] = keep.tile([P, PASSES, 2 * H], F32, name=kind + "_grouped", align_bytes=64)
+            w_codes[kind] = keep.tile([P, PASSES, H], U32, name=kind + "_codes", align_bytes=64)
+            w_scales[kind] = keep.tile([P, PASSES, H], U8, name=kind + "_scales", align_bytes=64)
+
+        def scale_context(n):
+            prepared[n] = work.tile([P, F], BF16, name="scaled", bufs=2 * RUN + LEAD + 2)
             nc.vector.tensor_tensor(
-                out=tile[:].rearrange("p (u w e) -> p u w e", u=2, e=2),
+                out=prepared[n][:].rearrange("p (u w e) -> p u w e", u=2, e=2),
                 in0=raw[units[n]].bitcast(FP8).rearrange("p (w u e) -> p u w e", u=2, e=2),
                 in1=spread[:].rearrange("p (u w e) -> p u w e", u=2, e=2),
                 op=MULT,
             )
-            scaled[n] = tile
 
-        def permute_unit(n):
-            kind, j, k = units[n]
-            if XPERM and kind == "x":
-                src = raw[("x", j)]
-                scaled[n] = work.tile([P, F], BF16, name="permuted", bufs=4)
-                nc.scalar.copy(
-                    out=scaled[n][:].bitcast(F32).rearrange("p (u q i) -> p u q i", u=2, i=1),
-                    in_=src[:].bitcast(F32).rearrange("p (q u i) -> p u q i", u=2, i=1),
-                )
-
-        def turn(n, src, permuted):
-            words = src.bitcast(F32)
-            bank = turn_bank(n)
-            for g in range(2):
-                for u in range(2):
-                    if permuted:
-                        cols = words[:, 256 * u + P * g : 256 * u + P * (g + 1)]
-                    else:
-                        cols = words[:, 256 * g + u : 256 * (g + 1) : 2]
-                    nc.tensor.transpose(bank[:, (2 * g + u) * P : (2 * g + u + 1) * P], cols, ident[:])
-            return bank[:].rearrange("p (g u r) -> p g r u", g=2, u=2)
-
-        def turn_unit(n):
-            kind, j, k = units[n]
-            if kind == "ctx":
-                banks[n] = turn(n, scaled[n][:], True)
-            elif kind == "x":
-                banks[n] = turn(n, scaled[n][:] if XPERM else raw[("x", j)][:], XPERM)
-            elif kind in ("wn", "wc"):
-                banks[n] = turn(n, scaled[n][:], True) if n in scaled else turn(n, raw[(kind, k)][:], False)
-            else:
-                banks[n] = turn(n, wu_raw[:].rearrange("p a h -> p (a h)"), False)
-
-        def group_weight(kind, t, bank):
-            dst = w_grouped[kind][:, :, 2 * P * t : 2 * P * (t + 1)].rearrange("p g (r u) -> p g r u", u=2)
-            nc.scalar.copy(out=dst, in_=bank)
-
-        def group_unit(n):
-            kind, j, k = units[n]
-            if kind in ("wn", "wc"):
-                group_weight(kind, k, banks[n])
-            else:
-                tile = work.tile([P, 512], F32, name="grouped", bufs=RUN + DLAG + 3, align_bytes=64)
-                nc.scalar.copy(out=tile[:].rearrange("p (g r u) -> p g r u", g=2, u=2), in_=banks[n])
-                grouped[n] = tile
-
-        def quantize_weight(kind):
-            for g in range(2):
-                nc.vector.quantize_mx(
-                    out=w_codes[kind][:, g, :].bitcast(FP8X4),
-                    scales=w_planes[kind][:, g, :],
-                    in_=w_grouped[kind][:, g, :].bitcast(BF16),
-                )
-
-        def quantize_unit(n):
-            kind, j, k = units[n]
-            if kind in ("wn", "wc"):
-                if k == 3:
-                    quantize_weight(kind)
-                return
-            pool, bufs = (keep, 1) if kind == "wu" else (work, 2 * RUN + 1)
-            codes[n] = pool.tile([P, 256], U32, name="codes", bufs=bufs, align_bytes=64)
-            planes[n] = pool.tile([P, 256], U8, name="plane", bufs=bufs, align_bytes=64)
-            nc.vector.quantize_mx(
-                out=codes[n][:].bitcast(FP8X4), scales=planes[n][:], in_=grouped[n][:].bitcast(BF16)
+        def reorder_x(n):
+            prepared[n] = work.tile([P, F], BF16, name="reordered", bufs=2)
+            nc.scalar.copy(
+                out=prepared[n][:].bitcast(F32).rearrange("p (u w) -> p u w", u=2),
+                in_=raw[units[n]].bitcast(F32).rearrange("p (w u) -> p u w", u=2),
             )
 
-        def multiply_unit(n):
-            kind = units[n][0]
-            if kind in ("wn", "wc", "wu"):
-                return
-            weight = "wc" if kind == "ctx" else "wn"
-            products[n] = prod_bank(len(products))
-            for g in range(2):
+        def turn(n):
+            bank = turn_bank(n)
+            for g in range(PASSES):
+                for u in range(2):
+                    if n in prepared:
+                        first = u * (WORDS // 2) + g * P
+                        words = prepared[n][:].bitcast(F32)[:, first : first + P]
+                    else:
+                        words = raw[units[n]].bitcast(F32)[:, 2 * P * g + u : 2 * P * (g + 1) : 2]
+                    nc.tensor.transpose(bank[:, (2 * g + u) * P : (2 * g + u + 1) * P], words, ident[:])
+            turned[n] = bank[:].rearrange("p (g u r) -> p g r u", g=PASSES, u=2)
+
+        def group(n):
+            kind, j, t = units[n]
+            if kind in w_grouped:
+                columns = w_grouped[kind][:, :, 2 * P * t : 2 * P * (t + 1)]
+                nc.scalar.copy(out=columns.rearrange("p g (r u) -> p g r u", u=2), in_=turned[n])
+            else:
+                grouped[n] = work.tile([P, WORDS], F32, name="grouped", bufs=RUN + 4, align_bytes=64)
+                nc.scalar.copy(out=grouped[n][:].rearrange("p (g r u) -> p g r u", g=PASSES, u=2), in_=turned[n])
+
+        def quantise(n):
+            kind, j, t = units[n]
+            if kind not in w_grouped:
+                pool, bufs = (keep, 1) if n == wu_unit else (work, 2 * RUN + 1)
+                codes[n] = pool.tile([P, PASSES * P], U32, name="codes", bufs=bufs, align_bytes=64)
+                scales[n] = pool.tile([P, PASSES * P], U8, name="scales", bufs=bufs, align_bytes=64)
+                nc.vector.quantize_mx(
+                    out=codes[n][:].bitcast(FP8X4), scales=scales[n][:], in_=grouped[n][:].bitcast(BF16)
+                )
+            elif t == PACK - 1:
+                for g in range(PASSES):
+                    nc.vector.quantize_mx(
+                        out=w_codes[kind][:, g, :].bitcast(FP8X4),
+                        scales=w_scales[kind][:, g, :],
+                        in_=w_grouped[kind][:, g, :].bitcast(BF16),
+                    )
+
+        def multiply(n):
+            kind = "wc" if units[n][0] == "ctx" else "wn"
+            products[n] = product_bank(len(products))
+            for g in range(PASSES):
                 nc.tensor.matmul_mx(
                     out=products[n][:],
                     lhsT=codes[n][:, g * P : (g + 1) * P].bitcast(FP8X4),
-                    lhsT_scale=planes[n][:, g * P : (g + 1) * P],
-                    rhs=w_codes[weight][:, g, :].bitcast(FP8X4),
-                    rhs_scale=w_planes[weight][:, g, :],
+                    lhsT_scale=scales[n][:, g * P : (g + 1) * P],
+                    rhs=w_codes[kind][:, g, :].bitcast(FP8X4),
+                    rhs_scale=w_scales[kind][:, g, :],
                     start=(g == 0),
-                    stop=(g == 1),
+                    stop=(g == PASSES - 1),
                 )
 
-        def weigh_unit(n):
+        def weigh(n):
             kind, j, k = units[n]
-            if kind in ("wn", "wc", "wu"):
-                return
             if kind == "x":
-                weighted[n] = work.tile([P, H], F32, name="x_product", bufs=XAHEAD + 3)
-            else:
-                weighted[n] = work.tile([P, H], F32, name="weighted", bufs=(SLAG + 1) * RUN + 2)
-            if n in folded:
+                weighed[n] = work.tile([P, H], F32, name="x_product", bufs=3)
+                nc.scalar.copy(out=weighed[n][:], in_=products[n][:])
+                return
+            weighed[n] = work.tile([P, H], F32, name="weighed", bufs=2 * RUN + 2)
+            gain = gains[:, K * j + k : K * j + k + 1]
+            if n in added_to:
                 nc.vector.scalar_tensor_tensor(
-                    out=weighted[n][:], in0=products[n][:], scalar=weights[:, K * j + k : K * j + k + 1],
-                    in1=weighted[folded[n]][:], op0=MULT, op1=ADD,
+                    out=weighed[n][:], in0=products[n][:], scalar=gain, in1=weighed[added_to[n]][:], op0=MULT, op1=ADD
                 )
-            elif kind == "x":
-                nc.scalar.copy(out=weighted[n][:], in_=products[n][:])
             else:
-                nc.scalar.activation(
-                    out=weighted[n][:], in_=products[n][:], func=COPY, scale=weights[:, K * j + k : K * j + k + 1]
-                )
+                nc.scalar.activation(out=weighed[n][:], in_=products[n][:], func=COPY, scale=gain)
 
-        sums, masked, h_grouped, h_codes, h_planes, results = {}, {}, {}, {}, {}, {}
+        h_sums, masked, h_grouped, h_codes, h_scales, results = {}, {}, {}, {}, {}, {}
 
-        def mask_weights(j):
+        def mask_gains(j):
             masked[j] = keep.tile([P, P], BF16, name="masked%d" % j)
-            nc.scalar.activation(out=masked[j][:], in_=weights_t[:], func=COPY, scale=row_mask[:, j : j + 1])
+            nc.scalar.activation(out=masked[j][:], in_=gains_turned[:], func=COPY, scale=row_mask[:, j : j + 1])
 
-        def sum_unit(n):
+        def add_bias_piece(j):
+            t, first, nodes = bias_pieces[j].pop(0)
+            nc.tensor.matmul(
+                h_sums[j][:, t * P + first : t * P + first + nodes],
+                lhsT=bias_cols[:, t * P : (t + 1) * P],
+                rhs=masked[j][:, first : first + nodes],
+                start=False,
+                stop=False,
+            )
+
+        def change_over():
+            waiting = [j for j in h_sums if bias_pieces[j]]
+            if waiting:
+                add_bias_piece(waiting[0])
+
+        def sum_term(n):
             j = units[n][1]
-            if j not in sums:
-                sums[j] = sum_bank(j, H)
-                for t in range(4):
-                    nc.tensor.matmul(
-                        sums[j][:, t * P : (t + 1) * P],
-                        lhsT=bias_cols[:, t * P : (t + 1) * P],
-                        rhs=masked[j][:],
-                        start=(t == 0),
-                        stop=False,
-                    )
-            terms[j].remove(n)
-            for t in range(4):
+            opens = j not in h_sums
+            if opens:
+                h_sums[j] = h_bank(j, H)
+            open_terms[j].remove(n)
+            while not open_terms[j] and bias_pieces[j]:
+                add_bias_piece(j)
+            for t in range(PACK):
                 nc.tensor.matmul(
-                    sums[j][:, t * P : (t + 1) * P],
-                    lhsT=weighted[n][:, t * P : (t + 1) * P],
+                    h_sums[j][:, t * P : (t + 1) * P],
+                    lhsT=weighed[n][:, t * P : (t + 1) * P],
                     rhs=ident[:],
                     is_transpose=True,
-                    start=False,
-                    stop=(not terms[j] and t == 3),
+                    start=(opens and t == 0),
+                    stop=(not open_terms[j] and t == PACK - 1),
                 )
 
         def group_h(j):
             h_grouped[j] = work.tile([P, H], BF16, name="h_grouped", bufs=2, align_bytes=64)
             nc.scalar.copy(
-                out=h_grouped[j][:].rearrange("p (r t) -> p r t", t=4),
-                in_=sums[j][:].rearrange("p (t r) -> p r t", t=4),
+                out=h_grouped[j][:].rearrange("p (r t) -> p r t", t=PACK),
+                in_=h_sums[j][:].rearrange("p (t r) -> p r t", t=PACK),
             )
 
-        def quantize_h(j):
+        def quantise_h(j):
             h_codes[j] = work.tile([P, P], U32, name="h_codes", bufs=2, align_bytes=64)
-            h_planes[j] = work.tile([P, P], U8, name="h_plane", bufs=2, align_bytes=64)
-            nc.vector.quantize_mx(out=h_codes[j][:].bitcast(FP8X4), scales=h_planes[j][:], in_=h_grouped[j][:])
+            h_scales[j] = work.tile([P, P], U8, name="h_scales", bufs=2, align_bytes=64)
+            nc.vector.quantize_mx(out=h_codes[j][:].bitcast(FP8X4), scales=h_scales[j][:], in_=h_grouped[j][:])
 
         def multiply_h(j):
-            wu_unit = units.index(("wu", 0, 0))
-            results[j] = sum_bank(j, H)
+            results[j] = h_bank(j, H)
             nc.tensor.matmul_mx(
                 out=results[j][:, 0:O],
                 lhsT=h_codes[j][:].bitcast(FP8X4),
-                lhsT_scale=h_planes[j][:],
+                lhsT_scale=h_scales[j][:],
                 rhs=codes[wu_unit][:].bitcast(FP8X4),
-                rhs_scale=planes[wu_unit][:],
+                rhs_scale=scales[wu_unit][:],
                 start=True,
                 stop=True,
             )
 
         def finish(j):
-            res = work.tile([P, O], F32, name="res", bufs=2)
-            nc.vector.tensor_tensor(out=res[:], in0=results[j][:, 0:O], in1=bu_rows[:], op=ADD)
-            nc.sync.dma_start(out=out_rows[:, j, :], in_=res[:])
-
-        weights_t = keep.tile([P, P], BF16, name="weights_t")
-        bias_cols = keep.tile([P, H], BF16, name="bias_cols")
-
-        def run(r):
-            return runs[r] if 0 <= r < len(runs) else []
+            out_tile = work.tile([P, O], F32, name="out_tile", bufs=2)
+            nc.vector.tensor_tensor(out=out_tile[:], in0=results[j][:, 0:O], in1=bu_rows[:], op=ADD)
+            nc.sync.dma_start(out=out_rows[:, j, :], in_=out_tile[:])
 
         n_scaled = len([n for n in ctx_units if n in runs[0]])
-        def permute_wc(n):
-            scaled[n] = work.tile([P, F], BF16, name="permuted", bufs=4)
-            nc.vector.tensor_copy(
-                out=scaled[n][:].bitcast(F32).rearrange("p (u w) -> p u w", u=2),
-                in_=raw[("wc", n)][:].bitcast(F32).rearrange("p (w u) -> p u w", u=2),
-            )
-
-        for n in range(4 - WCV, 4):
-            if WCV > 2 and n == 2:
-                scale_ctx(ctx_units[0])
-            permute_wc(n)
-        for n in ctx_units[(1 if WCV > 2 else 0):n_scaled]:
-            scale_ctx(n)
-        for n in run(0):
-            permute_unit(n)
+        for n in ctx_units[:n_scaled]:
+            scale_context(n)
+        n_quantised = 0
         closed = {}
-        n_quantized = 0
-        for it in range(-1, len(runs) + 5):
-            to_turn, to_sum = (run(it + 1) if it < DEEP_FROM else run(it + 1) + run(it + 2) if it == DEEP_FROM else run(it + 2)), summed_at.get(it, [])
-            if it == 0:
-                weights_bank = sum_bank(1, P)
-                nc.tensor.transpose(weights_bank[:], weights[:], ident[:])
-            for i in range(max(len(to_turn), len(to_sum) + GOFF)):
+        for step in range(-1, max(summed_at) + 3):
+            to_turn, to_sum = run(step + 1), summed_at.get(step, [])
+            change_over()
+            if step == 0:
+                gains_bank = h_bank(1, P)
+                nc.tensor.transpose(gains_bank[:], gains[:], ident[:])
+            for i in range(max(len(to_turn), len(to_sum) + 1)):
                 if i < len(to_turn):
-                    turn_unit(to_turn[i])
-                    group_unit(to_turn[i])
-                if 0 <= i - GOFF < len(to_sum):
-                    n = to_sum[i - GOFF]
-                    sum_unit(n)
-                    if not terms[units[n][1]]:
-                        group_h(units[n][1])
-                        closed[it] = units[n][1]
-            if it == 0:
-                nc.scalar.copy(out=weights_t[:], in_=weights_bank[:])
+                    turn(to_turn[i])
+                    group(to_turn[i])
+                if 1 <= i <= len(to_sum):
+                    j = units[to_sum[i - 1]][1]
+                    sum_term(to_sum[i - 1])
+                    if not open_terms[j]:
+                        group_h(j)
+                        closed[step] = j
+            if step == 0:
+                nc.scalar.copy(out=gains_turned[:], in_=gains_bank[:])
                 nc.scalar.copy(
-                    out=bias_cols[:].rearrange("p (t m) -> p t m", t=4),
-                    in_=bias_rows[:].rearrange("p (m t) -> p t m", t=4),
+                    out=bias_cols[:].rearrange("p (t m) -> p t m", t=PACK),
+                    in_=bias_rows[:].rearrange("p (m t) -> p t m", t=PACK),
                 )
-            for n in run(it):
-                if n in first_of_tile.values():
-                    mask_weights(units[n][1])
-            for n in (run(it + 2) if it + 1 < DEEP_FROM else run(it + 2) + run(it + 3) if it + 1 == DEEP_FROM else run(it + 3)):
-                permute_unit(n)
+            for n in run(step):
+                if units[n][0] == "ctx" and units[n][2] == 0:
+                    mask_gains(units[n][1])
+            for n in run(step + 2):
+                if units[n][0] == "x":
+                    reorder_x(n)
 
-            size = max(len(run(it + 1)), len(run(it + 2)))
-            need = len([n for n in ctx_units if n <= max((run(it + 3) if it + 1 >= DEEP_FROM else []) + run(it + 2) + run(it + 1) + [-1])])
-            goal = min(len(ctx_units), max(need, min(n_scaled + size, need + min(LEAD, max(0, it + RAMP)))))
-            to_scale = ctx_units[n_scaled:goal]
-            n_scaled = max(n_scaled, goal)
-            lag = DLAG if it >= 0 else 0
-            goal = max(max(to_turn + [-1]) + 1 - lag, max(run(it) + [-1]) + 1, n_quantized)
-            to_quantize = list(range(n_quantized, goal))
-            n_quantized = goal
-            if it - 1 in closed:
-                quantize_h(closed[it - 1])
-            slots = max(len(to_scale), len(to_quantize), 1)
+            needed = len([n for n in ctx_units if n <= max(run(step + 2) + to_turn + [-1])])
+            ahead = min(n_scaled + max(len(to_turn), len(run(step + 2))), needed + (LEAD if step > 0 else 0))
+            to_scale = ctx_units[n_scaled : max(needed, ahead)]
+            n_scaled = n_scaled + len(to_scale)
+            held_back = 1 if step >= 0 and to_scale else 0
+            goal = max(max(to_turn + [-1]) + 1 - held_back, max(run(step) + [-1]) + 1, n_quantised)
+            to_quantise = list(range(n_quantised, goal))
+            n_quantised = goal
+            if step - 1 in closed:
+                quantise_h(closed[step - 1])
+            slots = max(len(to_scale), len(to_quantise), 1)
             for i in range(slots):
                 if i < len(to_scale):
-                    scale_ctx(to_scale[i])
-                if it == -1 and i == 0:
+                    scale_context(to_scale[i])
+                if i == 0 and step == -1:
                     nc.vector.tensor_scalar(
-                        out=weights[:, 0:64], in0=attn_sb[:], scalar1=1.0 / K, scalar2=None, op0=MULT
+                        out=gains[:, 0:HALF], in0=attn_rows[:], scalar1=1.0 / K, scalar2=None, op0=MULT
                     )
-                if i == min(FPOS, slots - 1):
-                    for n in run(it - 1):
-                        if n in folded:
-                            weigh_unit(n)
-                if i == min(FIN, slots - 1) and it - 2 in closed:
-                    finish(closed[it - 2])
-                if i < len(to_quantize):
-                    quantize_unit(to_quantize[i])
+                if i == 0:
+                    for n in run(step - 1):
+                        if n in added_to:
+                            weigh(n)
+                if i == min(1, slots - 1) and step - 2 in closed:
+                    finish(closed[step - 2])
+                if i < len(to_quantise):
+                    quantise(to_quantise[i])
 
-            if it - 1 in closed:
-                multiply_h(closed[it - 1])
-            for n in run(it):
-                multiply_unit(n)
-                if n not in folded:
-                    weigh_unit(n)
+            change_over()
+            if step - 1 in closed:
+                multiply_h(closed[step - 1])
+            for n in run(step):
+                if has_product(n):
+                    multiply(n)
+                    if n not in added_to:
+                        weigh(n)

@@ -23,7 +23,7 @@ PACK = 4
 PASSES = F // (P * PACK)
 WORDS = F // 2
 HALF = P // 2
-CTX_PER_LOAD = 2
+PAIR = 2
 
 RUN = 3
 FIRST_RUNS = [5, 2]
@@ -58,7 +58,7 @@ def tile_nodeembeddinglayer_pa_t_kernel(
         ctx_rows = contexts_bytes.rearrange("(p j) k f -> p j (k f)", j=TILES)
         out_rows = out.rearrange("(p j) o -> p j o", j=TILES)
         weight_rows = {"wc": Wc.rearrange("(m t) f -> m t f", t=PACK), "wn": Wn.rearrange("(m t) f -> m t f", t=PACK)}
-        raw = {}
+        raw, ctx_pairs = {}, {}
 
         def load_rows(unit, src):
             tile = keep.tile([P, F], BF16, name="raw_%s_%d_%d" % unit)
@@ -70,10 +70,9 @@ def tile_nodeembeddinglayer_pa_t_kernel(
                 load_rows((kind, 0, t), weight_rows[kind][:, t, :])
 
         def load_contexts(j, k0):
-            tile = keep.tile([P, CTX_PER_LOAD * F], U8, name="ctx_bytes_%d_%d" % (j, k0))
-            nc.sync.dma_start(out=tile[:], in_=ctx_rows[:, j, k0 * F : (k0 + CTX_PER_LOAD) * F])
-            for i in range(CTX_PER_LOAD):
-                raw[("ctx", j, k0 + i)] = tile[:, i * F : (i + 1) * F]
+            tile = keep.tile([P, PAIR * F], U8, name="ctx_bytes_%d_%d" % (j, k0))
+            nc.sync.dma_start(out=tile[:], in_=ctx_rows[:, j, k0 * F : (k0 + PAIR) * F])
+            ctx_pairs[(j, k0)] = tile[:]
 
         scale_cols = keep.tile([P, 8], F32, name="scale_cols")
         nc.sync.dma_start(out=scale_cols[:], in_=contexts_scale.rearrange("a b (n m) -> (a b n) m", m=8))
@@ -96,11 +95,10 @@ def tile_nodeembeddinglayer_pa_t_kernel(
         nc.sync.dma_start(out=bu_rows[:], in_=bu.partition_broadcast(P))
         for j in range(1, TILES):
             load_rows(("x", j, 0), x_rows[:, j, :])
-            for k0 in range(0, K, CTX_PER_LOAD):
+            for k0 in range(0, K, PAIR):
                 load_contexts(j, k0)
 
-        spread = keep.tile([P, F], F32, name="spread")
-        spread_halves = spread[:].rearrange("p (u n s) -> p u n s", u=2, s=4)
+        spread = keep.tile([P, 2, PAIR, F // 2], F32, name="spread")
         scale_banks = []
         for u in range(2):
             bank = product_bank(u)
@@ -122,8 +120,9 @@ def tile_nodeembeddinglayer_pa_t_kernel(
         nc.vector.tensor_scalar(
             out=row_mask[:], in0=block_of_row[:, 0:TILES], scalar1=is_bn_row[:], scalar2=None, op0=ADD
         )
-        nc.scalar.copy(out=spread_halves[:, 0], in_=scale_banks[0])
-        nc.vector.tensor_copy(out=spread_halves[:, 1], in_=scale_banks[1])
+        for i in range(PAIR):
+            for u in range(2):
+                nc.scalar.copy(out=spread[:, u, i, :].rearrange("p (n s) -> p n s", s=4), in_=scale_banks[u])
         gains_turned = keep.tile([P, P], BF16, name="gains_turned")
         bias_cols = keep.tile([P, H], BF16, name="bias_cols")
 
@@ -161,7 +160,7 @@ def tile_nodeembeddinglayer_pa_t_kernel(
         pieces = [(t, first, HALF) for t in range(2) for first in (0, HALF)] + [(t, 0, P) for t in range(2, PACK)]
         bias_pieces = {j: list(pieces) for j in range(TILES)}
 
-        prepared, turned, grouped, codes, scales, products, weighed = {}, {}, {}, {}, {}, {}, {}
+        scaled, turned, grouped, codes, scales, products, weighed = {}, {}, {}, {}, {}, {}, {}
         w_grouped, w_codes, w_scales = {}, {}, {}
         for kind in ("wc", "wn"):
             w_grouped[kind] = keep.tile([P, PASSES, 2 * H], F32, name=kind + "_grouped", align_bytes=64)
@@ -169,28 +168,30 @@ def tile_nodeembeddinglayer_pa_t_kernel(
             w_scales[kind] = keep.tile([P, PASSES, H], U8, name=kind + "_scales", align_bytes=64)
 
         def scale_context(n):
-            prepared[n] = work.tile([P, F], BF16, name="scaled", bufs=2 * RUN + LEAD + 2)
-            nc.vector.tensor_tensor(
-                out=prepared[n][:].rearrange("p (u w e) -> p u w e", u=2, e=2),
-                in0=raw[units[n]].bitcast(FP8).rearrange("p (w u e) -> p u w e", u=2, e=2),
-                in1=spread[:].rearrange("p (u w e) -> p u w e", u=2, e=2),
-                op=MULT,
-            )
-
-        def reorder_x(n):
-            prepared[n] = work.tile([P, F], BF16, name="reordered", bufs=2)
-            nc.scalar.copy(
-                out=prepared[n][:].bitcast(F32).rearrange("p (u w) -> p u w", u=2),
-                in_=raw[units[n]].bitcast(F32).rearrange("p (w u) -> p u w", u=2),
-            )
+            kind, j, k = units[n]
+            if k % PAIR:
+                return
+            tile = work.tile([P, 2, PAIR, F // 2], BF16, name="scaled", bufs=RUN + 2)
+            values = ctx_pairs[(j, k)].bitcast(FP8).rearrange("p (i w u e) -> p u i w e", i=PAIR, u=2, e=2)
+            factors = spread[:].rearrange("p u i (w e) -> p u i w e", e=2)
+            rounded = tile[:].rearrange("p u i (w e) -> p u i w e", e=2)
+            if n == ctx_units[0]:
+                for i in range(PAIR):
+                    for u in range(2):
+                        nc.vector.tensor_tensor(
+                            out=rounded[:, u, i], in0=values[:, u, i], in1=factors[:, u, 0], op=MULT
+                        )
+            else:
+                nc.vector.tensor_tensor(out=rounded, in0=values, in1=factors, op=MULT)
+            for i in range(PAIR):
+                scaled[units.index((kind, j, k + i))] = tile[:, :, i, :]
 
         def turn(n):
             bank = turn_bank(n)
             for g in range(PASSES):
                 for u in range(2):
-                    if n in prepared:
-                        first = u * (WORDS // 2) + g * P
-                        words = prepared[n][:].bitcast(F32)[:, first : first + P]
+                    if n in scaled:
+                        words = scaled[n][:, u, :].bitcast(F32)[:, g * P : (g + 1) * P]
                     else:
                         words = raw[units[n]].bitcast(F32)[:, 2 * P * g + u : 2 * P * (g + 1) : 2]
                     nc.tensor.transpose(bank[:, (2 * g + u) * P : (2 * g + u + 1) * P], words, ident[:])
@@ -349,9 +350,6 @@ def tile_nodeembeddinglayer_pa_t_kernel(
             for n in run(step):
                 if units[n][0] == "ctx" and units[n][2] == 0:
                     mask_gains(units[n][1])
-            for n in run(step + 2):
-                if units[n][0] == "x":
-                    reorder_x(n)
 
             needed = len([n for n in ctx_units if n <= max(run(step + 2) + to_turn + [-1])])
             ahead = min(n_scaled + max(len(to_turn), len(run(step + 2))), needed + (LEAD if step > 0 else 0))

from contextlib import ExitStack

import concourse.mybir as mybir
from concourse.masks import make_identity

N, K, F, H, O = 1024, 8, 1024, 512, 256
FLOPS = 2 * (N * F * H + N * K * F * H + N * H * O)

F32 = mybir.dt.float32
BF16 = mybir.dt.bfloat16
U32 = mybir.dt.uint32
U8 = mybir.dt.uint8
FP8 = mybir.dt.float8_e4m3fn
FP8X4 = mybir.dt.float8_e4m3fn_x4
MULT = mybir.AluOpType.mult
ADD = mybir.AluOpType.add
COPY = mybir.ActivationFunctionType.Copy
AXIS_X = mybir.AxisListType.X

P = 128
TILES = N // P
PACK = 4
PASSES = F // (P * PACK)
WORDS = F // 2
HALF = P // 2
PAIR = 2

RUN = 3
FIRST_RUNS = [5, 2]
X_PLACE = 4
LEAD = 1
CHAINS = 2


def tile_nodeembeddinglayer_pa_t_kernel(
    tc, x, contexts_bytes, contexts_scale, attn, Wn, bn, Wc, bc, Wu, bu, out
):
    nc = tc.nc
    with ExitStack() as stack:
        keep = stack.enter_context(tc.tile_pool(name="keep", bufs=1))
        work = stack.enter_context(tc.tile_pool(name="work", bufs=1))
        psum = stack.enter_context(tc.psum_pool(name="psum", bufs=1))
        stack.enter_context(tc.manual_schedule())

        def turn_bank(i):
            return psum.tile([P, WORDS], F32, name="turn", tag="turn%d" % (i % RUN))

        def product_bank(i):
            return psum.tile([P, H], F32, name="product", tag="product%d" % (i % RUN))

        def h_bank(j, width):
            return psum.tile([P, width], F32, name="hsum", tag="hsum%d" % (j % 2))

        ident = keep.tile([P, P], F32, name="ident")
        make_identity(nc, ident[:])

        x_rows = x.rearrange("(p j) f -> p j f", j=TILES)
        ctx_rows = contexts_bytes.rearrange("(p j) k f -> p j (k f)", j=TILES)
        out_rows = out.rearrange("(p j) o -> p j o", j=TILES)
        weight_rows = {"wc": Wc.rearrange("(m t) f -> m t f", t=PACK), "wn": Wn.rearrange("(m t) f -> m t f", t=PACK)}
        raw, ctx_pairs = {}, {}

        def load_rows(unit, src):
            tile = keep.tile([P, F], BF16, name="raw_%s_%d_%d" % unit)
            nc.sync.dma_start(out=tile[:], in_=src)
            raw[unit] = tile[:]

        def load_weight(kind):
            for t in range(PACK):
                load_rows((kind, 0, t), weight_rows[kind][:, t, :])

        def load_contexts(j, k0):
            tile = keep.tile([P, PAIR * F], U8, name="ctx_bytes_%d_%d" % (j, k0))
            nc.sync.dma_start(out=tile[:], in_=ctx_rows[:, j, k0 * F : (k0 + PAIR) * F])
            ctx_pairs[(j, k0)] = tile[:]

        scale_cols = keep.tile([P, 8], F32, name="scale_cols")
        nc.sync.dma_start(out=scale_cols[:], in_=contexts_scale.rearrange("a b (n m) -> (a b n) m", m=8))
        load_contexts(0, 0)
        load_weight("wc")
        load_contexts(0, 2)
        attn_rows = keep.tile([P, TILES * K], BF16, name="attn_rows")
        nc.sync.dma_start(out=attn_rows[:], in_=attn.rearrange("(p j) k -> p (j k)", j=TILES))
        load_weight("wn")
        load_contexts(0, 4)
        bias_rows = keep.tile([P, H], BF16, name="bias_rows")
        nc.sync.dma_start(out=bias_rows[0:HALF, :], in_=bc.partition_broadcast(HALF))
        nc.sync.dma_start(out=bias_rows[HALF:P, :], in_=bn.partition_broadcast(HALF))
        load_rows(("x", 0, 0), x_rows[:, 0, :])
        load_contexts(0, 6)
        wu_rows = keep.tile([P, O // P, H], BF16, name="wu_rows")
        nc.sync.dma_start(out=wu_rows[:], in_=Wu.rearrange("(a p) c -> p a c", p=P))
        raw[("wu", 0, 0)] = wu_rows[:].rearrange("p a c -> p (a c)")
        bu_rows = keep.tile([P, O], BF16, name="bu_rows")
        nc.sync.dma_start(out=bu_rows[:], in_=bu.partition_broadcast(P))
        for j in range(1, TILES):
            load_rows(("x", j, 0), x_rows[:, j, :])
            for k0 in range(0, K, PAIR):
                load_contexts(j, k0)

        spread = keep.tile([P, 2, PAIR, F // 2], F32, name="spread")
        scale_banks = []
        for u in range(2):
            bank = product_bank(u)
            for s in range(4):
                m = 4 * (s // 2) + 2 * u + s % 2
                column = scale_cols[:, m : m + 1].to_broadcast([P, P])
                nc.tensor.transpose(bank[:, s * P : (s + 1) * P], column, ident[:])
            scale_banks.append(bank[:].rearrange("p (s n) -> p n s", s=4))

        block_of_row = keep.tile([P, P // K], F32, name="block_of_row")
        nc.vector.tensor_reduce(
            out=block_of_row[:], in_=ident[:].rearrange("p (b i) -> p b i", i=K), axis=AXIS_X, op=ADD
        )
        gains = keep.tile([P, P], F32, name="gains")
        nc.vector.memset(gains[:, HALF:P], 1.0 / HALF)
        is_bn_row = keep.tile([P, 1], F32, name="is_bn_row")
        nc.vector.tensor_reduce(out=is_bn_row[:], in_=ident[:, HALF:P], axis=AXIS_X, op=ADD)
        row_mask = keep.tile([P, TILES], F32, name="row_mask")
        nc.vector.tensor_scalar(
            out=row_mask[:], in0=block_of_row[:, 0:TILES], scalar1=is_bn_row[:], scalar2=None, op0=ADD
        )
        for i in range(PAIR):
            for u in range(2):
                nc.scalar.copy(out=spread[:, u, i, :].rearrange("p (n s) -> p n s", s=4), in_=scale_banks[u])
        gains_turned = keep.tile([P, P], BF16, name="gains_turned")
        bias_cols = keep.tile([P, H], BF16, name="bias_cols")

        units = [("wc", 0, t) for t in range(PACK)] + [("ctx", 0, 0), ("ctx", 0, 1)]
        for t in range(PACK):
            units = units + [("ctx", 0, t + 2), ("wn", 0, t)]
        units = units + [("wu", 0, 0), ("ctx", 0, 6), ("x", 0, 0), ("ctx", 0, 7)]
        for j in range(1, TILES):
            contexts = [("ctx", j, k) for k in range(K)]
            units = units + contexts[:X_PLACE] + [("x", j, 0)] + contexts[X_PLACE:]
        starts = [0, FIRST_RUNS[0]] + list(range(sum(FIRST_RUNS), len(units), RUN)) + [len(units)]
        runs = [list(range(starts[r], starts[r + 1])) for r in range(len(starts) - 1)]
        ctx_units = [n for n in range(len(units)) if units[n][0] == "ctx"]
        wu_unit = units.index(("wu", 0, 0))

        def run(r):
            return runs[r] if 0 <= r < len(runs) else []

        def has_product(n):
            return units[n][0] in ("ctx", "x")

        last_terms = [n for n in range(len(units)) if has_product(n) and units[n][1] == TILES - 1]
        added_to = {
            last_terms[i]: last_terms[i - CHAINS]
            for i in range(CHAINS, len(last_terms))
            if units[last_terms[i]][0] == "ctx"
        }
        open_terms = {j: [] for j in range(TILES)}
        summed_at = {}
        for r in range(len(runs)):
            for n in runs[r]:
                if has_product(n) and n not in added_to.values():
                    open_terms[units[n][1]].append(n)
                    summed_at.setdefault(r + (2 if n in added_to else 1), []).append(n)
        pieces = [(t, first, HALF) for t in range(2) for first in (0, HALF)] + [(t, 0, P) for t in range(2, PACK)]
        bias_pieces = {j: list(pieces) for j in range(TILES)}

        scaled, turned, grouped, codes, scales, products, weighed = {}, {}, {}, {}, {}, {}, {}
        w_grouped, w_codes, w_scales = {}, {}, {}
        for kind in ("wc", "wn"):
            w_grouped[kind] = keep.tile([P, PASSES, 2 * H], F32, name=kind + "_grouped", align_bytes=64)
            w_codes[kind] = keep.tile([P, PASSES, H], U32, name=kind + "_codes", align_bytes=64)
            w_scales[kind] = keep.tile([P, PASSES, H], U8, name=kind + "_scales", align_bytes=64)

        def scale_context(n):
            kind, j, k = units[n]
            if k % PAIR:
                return
            tile = work.tile([P, 2, PAIR, F // 2], BF16, name="scaled", bufs=RUN + 2)
            values = ctx_pairs[(j, k)].bitcast(FP8).rearrange("p (i w u e) -> p u i w e", i=PAIR, u=2, e=2)
            factors = spread[:].rearrange("p u i (w e) -> p u i w e", e=2)
            rounded = tile[:].rearrange("p u i (w e) -> p u i w e", e=2)
            if n == ctx_units[0]:
                for i in range(PAIR):
                    for u in range(2):
                        nc.vector.tensor_tensor(
                            out=rounded[:, u, i], in0=values[:, u, i], in1=factors[:, u, 0], op=MULT
                        )
            else:
                nc.vector.tensor_tensor(out=rounded, in0=values, in1=factors, op=MULT)
            for i in range(PAIR):
                scaled[units.index((kind, j, k + i))] = tile[:, :, i, :]

        def turn(n):
            bank = turn_bank(n)
            for g in range(PASSES):
                for u in range(2):
                    if n in scaled:
                        words = scaled[n][:, u, :].bitcast(F32)[:, g * P : (g + 1) * P]
                    else:
                        words = raw[units[n]].bitcast(F32)[:, 2 * P * g + u : 2 * P * (g + 1) : 2]
                    nc.tensor.transpose(bank[:, (2 * g + u) * P : (2 * g + u + 1) * P], words, ident[:])
            turned[n] = bank[:].rearrange("p (g u r) -> p g r u", g=PASSES, u=2)

        def group(n):
            kind, j, t = units[n]
            if kind in w_grouped:
                columns = w_grouped[kind][:, :, 2 * P * t : 2 * P * (t + 1)]
                nc.scalar.copy(out=columns.rearrange("p g (r u) -> p g r u", u=2), in_=turned[n])
            else:
                grouped[n] = work.tile([P, WORDS], F32, name="grouped", bufs=RUN + 4, align_bytes=64)
                nc.scalar.copy(out=grouped[n][:].rearrange("p (g r u) -> p g r u", g=PASSES, u=2), in_=turned[n])

        def quantise(n):
            kind, j, t = units[n]
            if kind not in w_grouped:
                pool, bufs = (keep, 1) if n == wu_unit else (work, 2 * RUN + 1)
                codes[n] = pool.tile([P, PASSES * P], U32, name="codes", bufs=bufs, align_bytes=64)
                scales[n] = pool.tile([P, PASSES * P], U8, name="scales", bufs=bufs, align_bytes=64)
                nc.vector.quantize_mx(
                    out=codes[n][:].bitcast(FP8X4), scales=scales[n][:], in_=grouped[n][:].bitcast(BF16)
                )
            elif t == PACK - 1:
                for g in range(PASSES):
                    nc.vector.quantize_mx(
                        out=w_codes[kind][:, g, :].bitcast(FP8X4),
                        scales=w_scales[kind][:, g, :],
                        in_=w_grouped[kind][:, g, :].bitcast(BF16),
                    )

        def multiply(n):
            kind = "wc" if units[n][0] == "ctx" else "wn"
            products[n] = product_bank(len(products))
            for g in range(PASSES):
                nc.tensor.matmul_mx(
                    out=products[n][:],
                    lhsT=codes[n][:, g * P : (g + 1) * P].bitcast(FP8X4),
                    lhsT_scale=scales[n][:, g * P : (g + 1) * P],
                    rhs=w_codes[kind][:, g, :].bitcast(FP8X4),
                    rhs_scale=w_scales[kind][:, g, :],
                    start=(g == 0),
                    stop=(g == PASSES - 1),
                )

        def weigh(n):
            kind, j, k = units[n]
            if kind == "x":
                weighed[n] = work.tile([P, H], F32, name="x_product", bufs=3)
                nc.scalar.copy(out=weighed[n][:], in_=products[n][:])
                return
            weighed[n] = work.tile([P, H], F32, name="weighed", bufs=2 * RUN + 2)
            gain = gains[:, K * j + k : K * j + k + 1]
            if n in added_to:
                nc.vector.scalar_tensor_tensor(
                    out=weighed[n][:], in0=products[n][:], scalar=gain, in1=weighed[added_to[n]][:], op0=MULT, op1=ADD
                )
            else:
                nc.scalar.activation(out=weighed[n][:], in_=products[n][:], func=COPY, scale=gain)

        h_sums, masked, h_grouped, h_codes, h_scales, results = {}, {}, {}, {}, {}, {}

        def mask_gains(j):
            masked[j] = keep.tile([P, P], BF16, name="masked%d" % j)
            nc.scalar.activation(out=masked[j][:], in_=gains_turned[:], func=COPY, scale=row_mask[:, j : j + 1])

        def add_bias_piece(j):
            t, first, nodes = bias_pieces[j].pop(0)
            nc.tensor.matmul(
                h_sums[j][:, t * P + first : t * P + first + nodes],
                lhsT=bias_cols[:, t * P : (t + 1) * P],
                rhs=masked[j][:, first : first + nodes],
                start=False,
                stop=False,
            )

        def change_over():
            waiting = [j for j in h_sums if bias_pieces[j]]
            if waiting:
                add_bias_piece(waiting[0])

        def sum_term(n):
            j = units[n][1]
            opens = j not in h_sums
            if opens:
                h_sums[j] = h_bank(j, H)
            open_terms[j].remove(n)
            while not open_terms[j] and bias_pieces[j]:
                add_bias_piece(j)
            for t in range(PACK):
                nc.tensor.matmul(
                    h_sums[j][:, t * P : (t + 1) * P],
                    lhsT=weighed[n][:, t * P : (t + 1) * P],
                    rhs=ident[:],
                    is_transpose=True,
                    start=(opens and t == 0),
                    stop=(not open_terms[j] and t == PACK - 1),
                )

        def group_h(j):
            h_grouped[j] = work.tile([P, H], BF16, name="h_grouped", bufs=2, align_bytes=64)
            nc.scalar.copy(
                out=h_grouped[j][:].rearrange("p (r t) -> p r t", t=PACK),
                in_=h_sums[j][:].rearrange("p (t r) -> p r t", t=PACK),
            )

        def quantise_h(j):
            h_codes[j] = work.tile([P, P], U32, name="h_codes", bufs=2, align_bytes=64)
            h_scales[j] = work.tile([P, P], U8, name="h_scales", bufs=2, align_bytes=64)
            nc.vector.quantize_mx(out=h_codes[j][:].bitcast(FP8X4), scales=h_scales[j][:], in_=h_grouped[j][:])

        def multiply_h(j):
            results[j] = h_bank(j, H)
            nc.tensor.matmul_mx(
                out=results[j][:, 0:O],
                lhsT=h_codes[j][:].bitcast(FP8X4),
                lhsT_scale=h_scales[j][:],
                rhs=codes[wu_unit][:].bitcast(FP8X4),
                rhs_scale=scales[wu_unit][:],
                start=True,
                stop=True,
            )

        def finish(j):
            out_tile = work.tile([P, O], F32, name="out_tile", bufs=2)
            nc.vector.tensor_tensor(out=out_tile[:], in0=results[j][:, 0:O], in1=bu_rows[:], op=ADD)
            nc.sync.dma_start(out=out_rows[:, j, :], in_=out_tile[:])

        n_scaled = len([n for n in ctx_units if n in runs[0]])
        for n in ctx_units[:n_scaled]:
            scale_context(n)
        n_quantised = 0
        closed = {}
        for step in range(-1, max(summed_at) + 3):
            to_turn, to_sum = run(step + 1), summed_at.get(step, [])
            change_over()
            if step == 0:
                gains_bank = h_bank(1, P)
                nc.tensor.transpose(gains_bank[:], gains[:], ident[:])
            for i in range(max(len(to_turn), len(to_sum) + 1)):
                if i < len(to_turn):
                    turn(to_turn[i])
                    group(to_turn[i])
                if 1 <= i <= len(to_sum):
                    j = units[to_sum[i - 1]][1]
                    sum_term(to_sum[i - 1])
                    if not open_terms[j]:
                        group_h(j)
                        closed[step] = j
            if step == 0:
                nc.scalar.copy(out=gains_turned[:], in_=gains_bank[:])
                nc.scalar.copy(
                    out=bias_cols[:].rearrange("p (t m) -> p t m", t=PACK),
                    in_=bias_rows[:].rearrange("p (m t) -> p t m", t=PACK),
                )
            for n in run(step):
                if units[n][0] == "ctx" and units[n][2] == 0:
                    mask_gains(units[n][1])

            needed = len([n for n in ctx_units if n <= max(run(step + 2) + to_turn + [-1])])
            ahead = min(n_scaled + max(len(to_turn), len(run(step + 2))), needed + (LEAD if step > 0 else 0))
            to_scale = ctx_units[n_scaled : max(needed, ahead)]
            n_scaled = n_scaled + len(to_scale)
            held_back = 1 if step >= 0 and to_scale else 0
            goal = max(max(to_turn + [-1]) + 1 - held_back, max(run(step) + [-1]) + 1, n_quantised)
            to_quantise = list(range(n_quantised, goal))
            n_quantised = goal
            if step - 1 in closed:
                quantise_h(closed[step - 1])
            slots = max(len(to_scale), len(to_quantise), 1)
            for i in range(slots):
                if i < len(to_scale):
                    scale_context(to_scale[i])
                if i == 0 and step == -1:
                    nc.vector.tensor_scalar(
                        out=gains[:, 0:HALF], in0=attn_rows[:], scalar1=1.0 / K, scalar2=None, op0=MULT
                    )
                if i == 0:
                    for n in run(step - 1):
                        if n in added_to:
                            weigh(n)
                if i == min(1, slots - 1) and step - 2 in closed:
                    finish(closed[step - 2])
                if i < len(to_quantise):
                    quantise(to_quantise[i])

            change_over()
            if step - 1 in closed:
                multiply_h(closed[step - 1])
            for n in run(step):
                if has_product(n):
                    multiply(n)
                    if n not in added_to:
                        weigh(n)
